import numpy as np
import ml_dtypes


def mxq(x, axis, fmt="e4m3"):
    dtype, down = {"e4m3": (ml_dtypes.float8_e4m3fn, 7), "e5m2": (ml_dtypes.float8_e5m2, 14)}[fmt]
    v = np.moveaxis(np.asarray(x, np.float32).astype(ml_dtypes.bfloat16).astype(np.float64), axis, -1)
    blocks = v.reshape(v.shape[:-1] + (-1, 32))
    amax = np.abs(blocks).max(-1, keepdims=True)
    byte = np.maximum(np.where(amax > 0, np.frexp(amax)[1] - 1 + 127, 0) - down, 1)
    scale = np.exp2(byte - 127.0)
    codes = (blocks / scale).astype(np.float32).astype(dtype).astype(np.float64)
    return np.moveaxis((codes * scale).reshape(v.shape), -1, axis)


WIDE = False


def mx_kscale(k):
    if not WIDE:
        return np.ones(k)
    levels = np.array([10, -10, 5, -5, 0])
    a = np.random.permutation(np.resize(levels, k // 512 * 4)).reshape(k // 512, 4)
    idx = np.arange(k)
    return np.exp2(a[idx // 512, idx % 128 // 32])


BF16 = ml_dtypes.bfloat16


def bf(x):
    return np.asarray(x, np.float32).astype(BF16)


def f64(x):
    return np.asarray(x).astype(np.float64)


N, X_DIM, Y_DIM, HID = 1024, 512, 512, 2048


def setup_inputs():
    s = mx_kscale(X_DIM)
    t, u = mx_kscale(HID), mx_kscale(HID)
    col = 0.6 + 0.6 * np.random.standard_normal(Y_DIM)
    return {
        "x_samples": bf(np.random.standard_normal((N, X_DIM)) * s),
        "y_samples": bf(np.random.standard_normal((N, Y_DIM)) + col),
        "mu_W1": bf(np.random.standard_normal((X_DIM, HID)) / np.sqrt(X_DIM) / s[:, None] * t),
        "mu_b1": bf(np.random.standard_normal(HID) * 0.8 * t),
        "mu_W2": bf(np.random.standard_normal((HID, Y_DIM)) * 1.2 / np.sqrt(HID) / t[:, None]),
        "mu_b2": bf(0.4 + 0.4 * np.random.standard_normal(Y_DIM)),
        "lv_W1": bf(np.random.standard_normal((X_DIM, HID)) / np.sqrt(X_DIM) / s[:, None] * u),
        "lv_b1": bf(np.random.standard_normal(HID) * 0.8 * u),
        "lv_W2": bf(np.random.standard_normal((HID, Y_DIM)) / np.sqrt(HID) / u[:, None]),
        "lv_b2": bf(0.3 + 0.4 * np.random.standard_normal(Y_DIM)),
    }


def reference(x_samples, y_samples, mu_W1, mu_b1, mu_W2, mu_b2, lv_W1, lv_b1, lv_W2, lv_b2):
    x = f64(x_samples)
    y = f64(y_samples)
    xq = mxq(x, 1, "e4m3")
    h_mu = np.maximum((xq @ mxq(f64(mu_W1), 0, "e4m3")) + f64(mu_b1), 0.0)
    mu = (mxq(h_mu, 1, "e4m3") @ mxq(f64(mu_W2), 0, "e4m3")) + f64(mu_b2)
    h_lv = np.maximum((xq @ mxq(f64(lv_W1), 0, "e4m3")) + f64(lv_b1), 0.0)
    logvar = np.tanh((mxq(h_lv, 1, "e4m3") @ mxq(f64(lv_W2), 0, "e4m3")) + f64(lv_b2))
    w = 0.5 * np.exp(-logvar)
    n = x.shape[0]
    pos_row = -(((mu - y) ** 2) * w).sum(axis=1)
    Sy = y.sum(axis=0)
    Sy2 = (y ** 2).sum(axis=0)
    neg_row = -(w * (n * mu ** 2 - 2.0 * mu * Sy + Sy2)).sum(axis=1) / (n * n)
    return pos_row, neg_row

@@ -1,0 +1,507 @@
+from contextlib import ExitStack
+
+import concourse.mybir as mybir
+from concourse.masks import make_identity
+
+FLOPS = 4 * 2 * 1024 * 512 * 2048
+
+BF16 = mybir.dt.bfloat16
+F32 = mybir.dt.float32
+U32 = mybir.dt.uint32
+U8 = mybir.dt.uint8
+FP8X4 = mybir.dt.float8_e4m3fn_x4
+ACT = mybir.ActivationFunctionType
+ALU = mybir.AluOpType
+
+P = 128
+NS = 1024
+MU = 0
+LV = 1
+
+BLOCKS = (512, 256, 256)
+OFFSETS = (0, 512, 768)
+UNITS = [(b, head, g) for b in range(len(BLOCKS)) for head in (MU, LV) for g in range(4)]
+SCALAR_REGROUP = ((2, MU, 1), (2, MU, 3))
+PAIR_ADD = (True, True, True)
+OPEN_EARLY = ((LV, 2),)
+
+RANK = {
+    "x1": -2.0, "y": 1.0, "y_step": 0.5, "ys": 11.0, "w1": 3.5, "w2mu": 6.0, "w2lv": 10.0, "w2_step": 0.5,
+    "h": 1.5, "l2": 2.5, "d_step": 2.0, "mu": 1.2, "lv": 2.7, "p": 1.9, "r": 1.0,
+}
+SLOTS = {"wraw": 5, "grpv": 3, "grps": 1, "hpl": 3, "hg": 3, "l1": 3, "l2": 4, "red": 1, "big": 3,
+         "dlt": 2, "th": 2, "wgt": 3, "p1": 3, "p2": 3, "s1": 2, "s2": 2, "res": 2}
+HANDOVER = 70
+ENGINES = ("dma", "pe", "act", "dve")
+
+
+def plan(records, slots):
+    users = {}
+    for r in records:
+        for key, tag in r["tiles"]:
+            users[key] = users.get(key, 0) + 1
+    done = {}
+    engine_of = {}
+    free_at = {}
+    taken = {}
+    released = {}
+    touched = {}
+    placed = set()
+    todo = list(records)
+    order = []
+    while todo:
+        best = None
+        for engine in ENGINES:
+            mine = [r for r in todo if r["engine"] == engine]
+            if engine == "dma":
+                mine = mine[:1]
+            ready = []
+            for r in mine:
+                t = 0.0
+                for n in r["needs"]:
+                    if n not in done:
+                        t = None
+                        break
+                    t = max(t, done[n] + (HANDOVER if engine_of[n] != engine else 0))
+                if t is None:
+                    continue
+                for key, tag in r["tiles"]:
+                    if key not in placed and taken.get(tag, 0) >= slots[tag]:
+                        if not released.get(tag):
+                            t = None
+                            break
+                        t = max(t, min(released[tag]) + HANDOVER)
+                if t is not None:
+                    ready.append((t, r))
+            if not ready:
+                continue
+            start = max(free_at.get(engine, 0.0), min(t for t, r in ready))
+            pick = min((r for t, r in ready if t <= start + 1e-9), key=lambda r: r["rank"])
+            if best is None or start < best[0]:
+                best = (start, pick)
+        assert best is not None, "the plan is stuck"
+        start, r = best
+        finish = start + r["cycles"]
+        free_at[r["engine"]] = finish
+        done[r["name"]] = finish + r["lag"]
+        engine_of[r["name"]] = r["engine"]
+        order.append((start, r["name"]))
+        todo = [q for q in todo if q["name"] != r["name"]]
+        for key, tag in r["tiles"]:
+            if key not in placed:
+                placed.add(key)
+                if taken.get(tag, 0) >= slots[tag]:
+                    first = min(released[tag])
+                    at = released[tag].index(first)
+                    released[tag] = released[tag][:at] + released[tag][at + 1 :]
+                else:
+                    taken[tag] = taken.get(tag, 0) + 1
+            users[key] = users[key] - 1
+            touched[key] = max(touched.get(key, 0.0), finish + r["lag"])
+            if users[key] == 0:
+                released[tag] = released.get(tag, []) + [touched[key]]
+    return order
+
+
+def tile_infoncemi_pa_kernel(
+    tc, x_samples, y_samples, mu_W1, mu_b1, mu_W2, mu_b2, lv_W1, lv_b1, lv_W2, lv_b2, out_0, out_1
+):
+    nc = tc.nc
+    w_dram = {(1, MU): mu_W1, (1, LV): lv_W1, (2, MU): mu_W2, (2, LV): lv_W2}
+    outs = (out_0, out_1)
+    records = []
+    emitters = {}
+
+    def op(name, engine, cycles, rank, needs, tiles, emit, lag=0):
+        records.append({"name": name, "engine": engine, "cycles": cycles, "rank": rank, "needs": needs,
+                        "tiles": tiles, "lag": lag})
+        emitters[name] = emit
+
+    tau = {}
+    clock = 0.0
+    for b, head, g in UNITS:
+        tau[(b, head, g)] = clock
+        clock += BLOCKS[b] / 512.0
+
+    def after(head, b):
+        return tau[(b, head, 3)] + BLOCKS[b] / 512.0
+
+    with ExitStack() as ctx:
+        const = ctx.enter_context(tc.tile_pool(name="const", bufs=1))
+        keep = ctx.enter_context(tc.tile_pool(name="keep", bufs=1))
+        pools = {}
+        for tag in ("wraw", "grpv", "grps", "hpl", "hg", "big", "dlt", "th", "wgt", "p1", "p2", "s1", "s2", "res"):
+            pools[tag] = ctx.enter_context(tc.tile_pool(name="pool_" + tag, bufs=SLOTS[tag]))
+        for tag in ("l1", "l2", "red"):
+            pools[tag] = ctx.enter_context(tc.psum_pool(name="psum_" + tag, bufs=SLOTS[tag]))
+        real = {}
+
+        def rot(key, tag, shape, dtype, align=None):
+            if key not in real:
+                if align is None:
+                    real[key] = pools[tag].tile(shape, dtype, tag=tag, name=key)
+                else:
+                    real[key] = pools[tag].tile(shape, dtype, tag=tag, name=key, align_bytes=align)
+            return real[key]
+
+        warm = const.tile([P, 1], F32)
+        nc.vector.memset(warm[:], 0.0)
+        warm2 = const.tile([P, 1], F32)
+        nc.scalar.activation(out=warm2[:], in_=warm[:], func=ACT.Tanh)
+        btile = const.tile([P, P], BF16)
+        nc.vector.memset(btile[:], 0.0)
+        nc.scalar.dma_start(out=btile[0:16, :], in_=mu_b1.rearrange("(r p) -> r p", p=P))
+        nc.scalar.dma_start(out=btile[16:32, :], in_=lv_b1.rearrange("(r p) -> r p", p=P))
+        nc.scalar.dma_start(out=btile[32:36, :], in_=mu_b2.rearrange("(r p) -> r p", p=P))
+        nc.scalar.dma_start(out=btile[36:40, :], in_=lv_b2.rearrange("(r p) -> r p", p=P))
+        ident_f = const.tile([P, P], F32)
+        make_identity(nc, ident_f[:])
+        ident_bf = const.tile([P, P], BF16)
+        make_identity(nc, ident_bf[:])
+        sel = []
+        for which, value in ((0, -0.5), (1, -0.5 / NS)):
+            s = const.tile([P, P], F32, name="sel%d" % which)
+            nc.vector.memset(s[:], 0.0)
+            nc.vector.memset(s[:, which : which + 1], value)
+            sel.append(s)
+        bias_sb = const.tile([P, 40], F32)
+        sy = const.tile([P, 4], F32)
+        negc = const.tile([P, 4], F32)
+        ebias = const.tile([P, 4], F32)
+        vsum = const.tile([P, 4], F32)
+        vn = const.tile([P, 4], F32)
+        junk = const.tile([P, 1024], BF16)
+
+        xc = keep.tile([P, 1024], U32, align_bytes=64)
+        xs = keep.tile([P, 1024], U8, align_bytes=64)
+        y_t = keep.tile([P, 4096], BF16)
+        wc = {}
+        ws = {}
+        hc = {}
+        hs = {}
+        for layer in (1, 2):
+            for head in (MU, LV):
+                wc[(layer, head)] = keep.tile([P, 2048], U32, align_bytes=64, name="wc%d%d" % (layer, head))
+                ws[(layer, head)] = keep.tile([P, 2048], U8, align_bytes=64, name="ws%d%d" % (layer, head))
+        for head in (MU, LV):
+            for b in range(len(BLOCKS)):
+                hc[(head, b)] = keep.tile([P, 4 * BLOCKS[b]], U32, align_bytes=64, name="hc%d%d" % (head, b))
+                hs[(head, b)] = keep.tile([P, 4 * BLOCKS[b]], U8, align_bytes=64, name="hs%d%d" % (head, b))
+
+        def regroup(engine, dst, src, width):
+            d = dst.rearrange("p (c i t) -> p c t i", i=4, t=4)
+            s = src.rearrange("p (t c i) -> p c t i", t=4, i=4)
+            if engine == "act":
+                nc.scalar.copy(out=d, in_=s)
+            else:
+                nc.vector.tensor_copy(out=d, in_=s)
+
+        def quantise(codes, plane, grouped):
+            nc.vector.quantize_mx(out=codes.bitcast(FP8X4), scales=plane, in_=grouped)
+
+        XRAW = ("x_raw", "big")
+        XG = ("x_grouped", "big")
+        YRAW = ("y_raw", "big")
+
+        def big(key):
+            return rot(key, "big", [P, 4096], BF16, 64)
+
+        def load_rows(key, src, half):
+            nc.sync.dma_start(
+                out=big(key)[:, half * 2048 : (half + 1) * 2048].rearrange("p (r k) -> p r k", r=4),
+                in_=src[half * 512 : (half + 1) * 512, :].rearrange("(r p) k -> p r k", p=P),
+            )
+
+        def x_transposes(half, pair):
+            r0 = half * 4 + pair * 2
+            xt = rot("xt%d%d" % (half, pair), "l1", [P, 512], F32)
+            words = big("x_raw")[:].bitcast(F32)
+            for rr in range(2):
+                for u in range(2):
+                    nc.tensor.transpose(
+                        xt[:, (rr * 2 + u) * P : (rr * 2 + u + 1) * P],
+                        words[:, (r0 + rr) * 256 + u * P : (r0 + rr) * 256 + (u + 1) * P],
+                        ident_f[:],
+                    )
+
+        def x_copy(half, pair):
+            r0 = half * 4 + pair * 2
+            nc.scalar.copy(
+                out=big("x_grouped")[:].bitcast(F32)[:, r0 * 256 : r0 * 256 + 512].rearrange(
+                    "p (r n u) -> p r n u", r=2, u=2
+                ),
+                in_=real["xt%d%d" % (half, pair)][:].rearrange("p (r u n) -> p r n u", r=2, u=2),
+            )
+
+        def x_quantise(half):
+            sl = slice(half * 512, (half + 1) * 512)
+            quantise(xc[:, sl], xs[:, sl], big("x_grouped")[:, half * 2048 : (half + 1) * 2048])
+
+        for half in range(2):
+            rank = -10.0 if half == 0 else RANK["x1"]
+            op("ld:x%d" % half, "dma", 1300, 0, [], [XRAW], lambda half=half: load_rows("x_raw", x_samples, half), 2300)
+            for pair in range(2):
+                bank = ("xt%d%d" % (half, pair), "l1")
+                op("xt:%d:%d" % (half, pair), "pe", 312, rank, ["ld:x%d" % half], [XRAW, bank],
+                   lambda half=half, pair=pair: x_transposes(half, pair), 120)
+                op("xc:%d:%d" % (half, pair), "act", 522, rank, ["xt:%d:%d" % (half, pair)], [bank, XG],
+                   lambda half=half, pair=pair: x_copy(half, pair))
+            op("xq:%d" % half, "dve", 526, rank, ["xc:%d:0" % half, "xc:%d:1" % half], [XG],
+               lambda half=half: x_quantise(half), 240)
+
+        def y_transposes(dt):
+            yps = rot("yps%d" % dt, "l2", [P, 1024], BF16)
+            for r in range(8):
+                nc.tensor.transpose(
+                    yps[:, r * P : (r + 1) * P], big("y_raw")[:, r * 512 + dt * P : r * 512 + (dt + 1) * P], ident_bf[:]
+                )
+
+        def y_copy(dt):
+            nc.scalar.activation(out=y_t[:, dt * 1024 : (dt + 1) * 1024], in_=real["yps%d" % dt][:], func=ACT.Copy,
+                                 accum_out=sy[:, dt : dt + 1])
+
+        def y_centre():
+            nc.vector.tensor_scalar(out=negc[:], in0=sy[:], scalar1=-1.0 / NS, scalar2=None, op0=ALU.mult)
+            nc.vector.tensor_tensor(out=ebias[:], in0=bias_sb[:, 32:36], in1=negc[:], op=ALU.add)
+
+        def y_spread(dt):
+            nc.scalar.activation(out=junk[:], in_=y_t[:, dt * 1024 : (dt + 1) * 1024], func=ACT.Square,
+                                 bias=negc[:, dt : dt + 1], accum_out=vsum[:, dt : dt + 1])
+
+        def y_variance():
+            nc.vector.tensor_scalar(out=vn[:], in0=vsum[:], scalar1=1.0 / NS, scalar2=None, op0=ALU.mult)
+
+        for half in range(2):
+            op("ld:y%d" % half, "dma", 1300, 0, [], [YRAW], lambda half=half: load_rows("y_raw", y_samples, half), 2300)
+        for dt in range(4):
+            bank = ("yps%d" % dt, "l2")
+            op("yt:%d" % dt, "pe", 500, RANK["y"] + dt * RANK["y_step"], ["ld:y0", "ld:y1"], [YRAW, bank],
+               lambda dt=dt: y_transposes(dt), 120)
+            op("yc:%d" % dt, "act", 1060, RANK["y"] + dt * RANK["y_step"], ["yt:%d" % dt], [bank],
+               lambda dt=dt: y_copy(dt))
+            op("ys:%d" % dt, "act", 1060, RANK["ys"] + dt * RANK["y_step"], ["ycn"], [], lambda dt=dt: y_spread(dt))
+        op("ycn", "dve", 140, RANK["y"] + 4 * RANK["y_step"], ["yc:%d" % dt for dt in range(4)], [], y_centre)
+        op("yv", "dve", 70, RANK["ys"] + 4 * RANK["y_step"], ["ys:%d" % dt for dt in range(4)], [], y_variance)
+
+        def w_name(layer, head, g):
+            return "%d%d%d" % (layer, head, g)
+
+        def w_rank(layer, head, g):
+            if layer == 1:
+                return tau[(0, head, g)] - RANK["w1"]
+            return (RANK["w2mu"] if head == MU else RANK["w2lv"]) + g * RANK["w2_step"]
+
+        def w_load(layer, head, g):
+            raw = rot("raw" + w_name(layer, head, g), "wraw", [P, 2048], BF16)
+            r3 = raw[:].rearrange("p (t c) -> p t c", t=4)
+            if layer == 1:
+                src = w_dram[(1, head)].rearrange("(u q e) c -> u q e c", u=2, e=2)
+                for u in range(2):
+                    nc.sync.dma_start(out=r3[:, 2 * u : 2 * u + 2, :], in_=src[u, :, :, g * 512 : (g + 1) * 512])
+            else:
+                nc.sync.dma_start(
+                    out=r3, in_=w_dram[(2, head)][g * 512 : (g + 1) * 512, :].rearrange("(t p) d -> p t d", p=P)
+                )
+
+        def w_regroup(layer, head, g, engine, tag):
+            n = w_name(layer, head, g)
+            regroup(engine, rot("grp" + n, tag, [P, 2048], BF16, 64)[:], real["raw" + n][:], 512)
+
+        def w_quantise(layer, head, g):
+            sl = slice(g * 512, (g + 1) * 512)
+            quantise(wc[(layer, head)][:, sl], ws[(layer, head)][:, sl], real["grp" + w_name(layer, head, g)][:])
+
+        chunks = sorted([(w_rank(layer, head, g), layer, head, g) for layer in (1, 2) for head in (MU, LV) for g in range(4)])
+        first_loads = ["ld:x0", "ld:w" + w_name(*chunks[0][1:]), "ld:x1", "ld:w" + w_name(*chunks[1][1:]), "ld:y0", "ld:y1"]
+        for rank, layer, head, g in chunks:
+            n = w_name(layer, head, g)
+            on_act = (layer, head, g) in SCALAR_REGROUP
+            raw = ("raw" + n, "wraw")
+            grp = ("grp" + n, "grps" if on_act else "grpv")
+            op("ld:w" + n, "dma", 1300, 0, [], [raw], lambda layer=layer, head=head, g=g: w_load(layer, head, g), 2300)
+            op("wr:" + n, "act" if on_act else "dve", 2058 if on_act else 1042, rank, ["ld:w" + n], [raw, grp],
+               lambda layer=layer, head=head, g=g, e=("act" if on_act else "dve"), tag=grp[1]: w_regroup(layer, head, g, e, tag))
+            op("wq:" + n, "dve", 526, rank, ["wr:" + n], [grp],
+               lambda layer=layer, head=head, g=g: w_quantise(layer, head, g), 240)
+
+        def l1_pass(b, head, g, t):
+            w = BLOCKS[b]
+            acc = rot("a%d%d%d%d" % (b, head, g, t), "l1", [P, w], F32)
+            csl = slice(g * 512 + t * P, g * 512 + (t + 1) * P)
+            nsl = slice(OFFSETS[b], OFFSETS[b] + w)
+            nc.tensor.matmul_mx(out=acc[:], lhsT=wc[(1, head)][:, csl].bitcast(FP8X4), lhsT_scale=ws[(1, head)][:, csl],
+                                rhs=xc[:, nsl].bitcast(FP8X4), rhs_scale=xs[:, nsl], start=True, stop=True)
+
+        def l1_exit(b, head, g, t):
+            w = BLOCKS[b]
+            hpl = rot("hpl%d%d%d" % (b, head, g), "hpl", [P, 4 * w], BF16)
+            col = head * 16 + g * 4 + t
+            nc.scalar.activation(out=hpl[:, t * w : (t + 1) * w], in_=real["a%d%d%d%d" % (b, head, g, t)][:], func=ACT.Relu,
+                                 bias=bias_sb[:, col : col + 1])
+
+        def h_regroup(b, head, g):
+            w = BLOCKS[b]
+            regroup("dve", rot("hg%d%d%d" % (b, head, g), "hg", [P, 4 * w], BF16, 64)[:], real["hpl%d%d%d" % (b, head, g)][:], w)
+
+        def h_quantise(b, head, g):
+            w = BLOCKS[b]
+            sl = slice(g * w, (g + 1) * w)
+            quantise(hc[(head, b)][:, sl], hs[(head, b)][:, sl], real["hg%d%d%d" % (b, head, g)][:])
+
+        previous = None
+        for b, head, g in UNITS:
+            w = BLOCKS[b]
+            u = "%d%d%d" % (b, head, g)
+            hpl = ("hpl" + u, "hpl")
+            hg = ("hg" + u, "hg")
+            for t in range(4):
+                bank = ("a%s%d" % (u, t), "l1")
+                needs = ["wq:" + w_name(1, head, g), "xq:%d" % (1 if OFFSETS[b] >= 512 else 0)]
+                if previous is not None:
+                    needs.append(previous)
+                previous = "l1:%s:%d" % (u, t)
+                op(previous, "pe", max(w / 2.0 + 8, 74), tau[(b, head, g)] + 0.01 * t, needs, [bank],
+                   lambda b=b, head=head, g=g, t=t: l1_pass(b, head, g, t), 200)
+                op("ex:%s:%d" % (u, t), "act", w + 10, tau[(b, head, g)] + 0.01 * t, [previous], [bank, hpl],
+                   lambda b=b, head=head, g=g, t=t: l1_exit(b, head, g, t))
+            op("hr:" + u, "dve", 2 * w + 18, tau[(b, head, g)] + RANK["h"], ["ex:%s:%d" % (u, t) for t in range(4)], [hpl, hg],
+               lambda b=b, head=head, g=g: h_regroup(b, head, g))
+            op("hq:" + u, "dve", w + 14, tau[(b, head, g)] + RANK["h"], ["hr:" + u], [hg],
+               lambda b=b, head=head, g=g: h_quantise(b, head, g), 240)
+
+        def l2_pass(head, b, dt, g):
+            w = BLOCKS[b]
+            acc = rot("o%d%d%d" % (head, b, dt), "l2", [P, w], F32)
+            wsl = slice(g * 512 + dt * P, g * 512 + (dt + 1) * P)
+            hsl = slice(g * w, (g + 1) * w)
+            nc.tensor.matmul_mx(out=acc[:], lhsT=wc[(2, head)][:, wsl].bitcast(FP8X4), lhsT_scale=ws[(2, head)][:, wsl],
+                                rhs=hc[(head, b)][:, hsl].bitcast(FP8X4), rhs_scale=hs[(head, b)][:, hsl],
+                                start=(g == 0), stop=(g == 3))
+
+        def kept(kind, b, dt):
+            w = BLOCKS[b]
+            if b == 0:
+                return rot("kept%s0" % kind, "big", [P, 2048], F32, 64)[:, dt * w : (dt + 1) * w]
+            base = 0 if kind == "e" else 1024
+            return rot("kept%d" % b, "big", [P, 2048], F32, 64)[:, base + dt * w : base + (dt + 1) * w]
+
+        def kept_key(kind, b):
+            return ("kept%s0" % kind if b == 0 else "kept%d" % b, "big")
+
+        def mu_delta(b, dt):
+            w = BLOCKS[b]
+            nc.vector.scalar_tensor_tensor(
+                out=rot("dlt%d%d" % (b, dt), "dlt", [P, w], F32)[:], in0=real["o%d%d%d" % (MU, b, dt)][:],
+                scalar=bias_sb[:, 32 + dt : 33 + dt], in1=y_t[:, dt * 1024 + OFFSETS[b] : dt * 1024 + OFFSETS[b] + w],
+                op0=ALU.add, op1=ALU.subtract)
+
+        def mu_centred_square(b, dt):
+            nc.scalar.activation(out=kept("e", b, dt), in_=real["o%d%d%d" % (MU, b, dt)][:], func=ACT.Square,
+                                 bias=ebias[:, dt : dt + 1])
+
+        def mu_delta_square(b, dt):
+            nc.scalar.activation(out=kept("s", b, dt), in_=real["dlt%d%d" % (b, dt)][:], func=ACT.Square)
+
+        def lv_tanh(b, dt):
+            nc.scalar.activation(out=rot("th%d%d" % (b, dt), "th", [P, BLOCKS[b]], F32)[:], in_=real["o%d%d%d" % (LV, b, dt)][:],
+                                 func=ACT.Tanh, bias=bias_sb[:, 36 + dt : 37 + dt])
+
+        def lv_exp(b, dt):
+            nc.scalar.activation(out=rot("wgt%d%d" % (b, dt), "wgt", [P, BLOCKS[b]], F32)[:], in_=real["th%d%d" % (b, dt)][:],
+                                 func=ACT.Exp, scale=-1.0)
+
+        def product(which, b, dt):
+            out = rot("p%d%d%d" % (which, b, dt), "p%d" % which, [P, BLOCKS[b]], F32)
+            if which == 1:
+                nc.vector.tensor_tensor(out=out[:], in0=kept("s", b, dt), in1=real["wgt%d%d" % (b, dt)][:], op=ALU.mult)
+            else:
+                nc.vector.scalar_tensor_tensor(out=out[:], in0=kept("e", b, dt), scalar=vn[:, dt : dt + 1],
+                                               in1=real["wgt%d%d" % (b, dt)][:], op0=ALU.add, op1=ALU.mult)
+
+        def pair_sum(which, b, dt):
+            nc.vector.tensor_tensor(out=rot("s%d%d%d" % (which, b, dt), "s%d" % which, [P, BLOCKS[b]], F32)[:],
+                                    in0=real["p%d%d%d" % (which, b, dt - 1)][:], in1=real["p%d%d%d" % (which, b, dt)][:], op=ALU.add)
+
+        def reduce_d(which, b, dt, src, first, last):
+            nc.tensor.matmul(out=rot("red%d" % b, "red", [P, BLOCKS[b]], F32)[:], lhsT=sel[which - 1][:], rhs=real[src][:],
+                             start=first, stop=last)
+
+        def result(b):
+            nc.scalar.copy(out=rot("res%d" % b, "res", [P, BLOCKS[b]], F32)[:], in_=real["red%d" % b][:])
+
+        def store(b):
+            for which in range(2):
+                nc.sync.dma_start(out=outs[which][OFFSETS[b] : OFFSETS[b] + BLOCKS[b]].rearrange("(o n) -> o n", o=1),
+                                  in_=real["res%d" % b][which : which + 1, :])
+
+        for b in range(len(BLOCKS)):
+            w = BLOCKS[b]
+            step = RANK["d_step"] * w / 512.0
+            red = ("red%d" % b, "red")
+            reduces = []
+            for dt in range(4):
+                for head in (MU, LV):
+                    bank = ("o%d%d%d" % (head, b, dt), "l2")
+                    for g in range(4):
+                        needs = ["wq:" + w_name(2, head, g), "hq:%d%d%d" % (b, head, g)]
+                        if g > 0:
+                            needs.append("l2:%d%d%d:%d" % (head, b, dt, g - 1))
+                        elif (head, b) not in OPEN_EARLY:
+                            needs.extend(["wq:" + w_name(2, head, 3), "hq:%d%d%d" % (b, head, 3)])
+                        op("l2:%d%d%d:%d" % (head, b, dt, g), "pe", max(w / 2.0 + 8, 74), after(head, b) + RANK["l2"] + dt * step,
+                           needs, [bank], lambda head=head, b=b, dt=dt, g=g: l2_pass(head, b, dt, g), 200)
+                n = "%d%d" % (b, dt)
+                mbank = ("o%d%d%d" % (MU, b, dt), "l2")
+                lbank = ("o%d%d%d" % (LV, b, dt), "l2")
+                rank = after(MU, b) + RANK["mu"] + dt * step
+                op("md:" + n, "dve", w + 15, rank, ["l2:%d%d%d:3" % (MU, b, dt), "yc:%d" % dt], [mbank, ("dlt" + n, "dlt")],
+                   lambda b=b, dt=dt: mu_delta(b, dt))
+                op("me:" + n, "act", w + 10, rank, ["l2:%d%d%d:3" % (MU, b, dt), "ycn"], [mbank, kept_key("e", b)],
+                   lambda b=b, dt=dt: mu_centred_square(b, dt))
+                op("ms:" + n, "act", w + 10, rank, ["md:" + n], [("dlt" + n, "dlt"), kept_key("s", b)],
+                   lambda b=b, dt=dt: mu_delta_square(b, dt))
+                rank = after(LV, b) + RANK["lv"] + dt * step
+                op("lt:" + n, "act", w + 10, rank, ["l2:%d%d%d:3" % (LV, b, dt)], [lbank, ("th" + n, "th")],
+                   lambda b=b, dt=dt: lv_tanh(b, dt))
+                op("lx:" + n, "act", w + 10, rank, ["lt:" + n], [("th" + n, "th"), ("wgt" + n, "wgt")],
+                   lambda b=b, dt=dt: lv_exp(b, dt))
+                for which in (1, 2):
+                    rank = after(LV, b) + RANK["p"] + dt * step
+                    pk = ("p%d%s" % (which, n), "p%d" % which)
+                    needs = ["lx:" + n, "ms:" + n] if which == 1 else ["lx:" + n, "me:" + n, "yv"]
+                    op("p%d:%s" % (which, n), "dve", w + 15, rank, needs,
+                       [pk, ("wgt" + n, "wgt"), kept_key("s" if which == 1 else "e", b)],
+                       lambda which=which, b=b, dt=dt: product(which, b, dt))
+                    rrank = after(LV, b) + RANK["r"] + dt * step
+                    first = which == 1 and dt == (1 if PAIR_ADD[b] else 0)
+                    last = which == 2 and dt == 3
+                    if not PAIR_ADD[b]:
+                        op("r%d:%s" % (which, n), "pe", 2 * w, rrank, ["p%d:%s" % (which, n)] + reduces[-1:], [pk, red],
+                           lambda which=which, b=b, dt=dt, first=first, last=last: reduce_d(
+                               which, b, dt, "p%d%d%d" % (which, b, dt), first, last), 200)
+                        reduces.append("r%d:%s" % (which, n))
+                    elif dt % 2 == 1:
+                        sk = ("s%d%s" % (which, n), "s%d" % which)
+                        op("a%d:%s" % (which, n), "dve", w + 15, rank, ["p%d:%s" % (which, n), "p%d:%d%d" % (which, b, dt - 1)],
+                           [pk, ("p%d%d%d" % (which, b, dt - 1), "p%d" % which), sk],
+                           lambda which=which, b=b, dt=dt: pair_sum(which, b, dt))
+                        op("r%d:%s" % (which, n), "pe", 2 * w, rrank, ["a%d:%s" % (which, n)] + reduces[-1:], [sk, red],
+                           lambda which=which, b=b, dt=dt, first=first, last=last: reduce_d(
+                               which, b, dt, "s%d%d%d" % (which, b, dt), first, last), 200)
+                        reduces.append("r%d:%s" % (which, n))
+            rank = after(LV, b) + RANK["r"] + 4 * step
+            op("res:%d" % b, "act", w + 10, rank, reduces[-1:], [red, ("res%d" % b, "res")], lambda b=b: result(b))
+            op("st:%d" % b, "dma", 20, rank, ["res:%d" % b], [("res%d" % b, "res")], lambda b=b: store(b), 2300)
+
+        loads = [r for r in records if r["engine"] == "dma"]
+        rest = [r for r in records if r["engine"] != "dma"]
+        head_loads = [r for n in first_loads for r in loads if r["name"] == n]
+        tail_loads = [r for r in loads if r["name"] not in first_loads]
+        order = plan(head_loads + tail_loads + rest, SLOTS)
+
+        with tc.manual_schedule():
+            bt_ps = pools["red"].tile([P, P], BF16, tag="red", name="bias_t")
+            nc.tensor.transpose(bt_ps[:], btile[:], ident_bf[:])
+            nc.vector.tensor_copy(out=bias_sb[:], in_=bt_ps[:, 0:40])
+            for start, name in order:
+                emitters[name]()

@@ -19,19 +19,17 @@ MU = 0
 LV = 1
 
 BLOCKS = (512, 256, 256)
-OFFSETS = (0, 512, 768)
+OFFSETS = tuple(sum(BLOCKS[:b]) for b in range(len(BLOCKS)))
 UNITS = [(b, head, g) for b in range(len(BLOCKS)) for head in (MU, LV) for g in range(4)]
 SCALAR_REGROUP = ((2, MU, 1), (2, MU, 3))
 PAIR_ADD = (True, True, True)
 OPEN_EARLY = ((LV, 2),)
 
-RANK = {
-    "x1": -2.0, "y": 1.0, "y_step": 0.5, "ys": 11.0, "w1": 3.5, "w2mu": 6.0, "w2lv": 10.0, "w2_step": 0.5,
-    "h": 1.5, "l2": 2.5, "d_step": 2.0, "mu": 1.2, "lv": 2.7, "p": 1.9, "r": 1.0,
-}
-SLOTS = {"wraw": 5, "grpv": 3, "grps": 1, "hpl": 3, "hg": 3, "l1": 3, "l2": 4, "red": 1, "big": 3,
+RANK = {"bias": -5, "x1": -2, "y": 1, "y_step": -2, "ys": 11, "w1": 3.5, "w2mu": 4.5, "w2lv": 11.1, "w2_step": 0.5, "h": 5.5, "l2": 3, "d_step": 1.8, "mu": 5.2, "lv": 3.7, "p": 1.9, "r": 3}
+SLOTS = {"wraw": 5, "grpv": 3, "grps": 1, "hpl": 4, "hg": 3, "l1": 4, "l2": 3, "red": 1, "big": 3,
          "dlt": 2, "th": 2, "wgt": 3, "p1": 3, "p2": 3, "s1": 2, "s2": 2, "res": 2}
-HANDOVER = 70
+HANDOVER = 320
+RESULT_LAG = {"dma": 2300, "pe": 200, "act": 240, "dve": 240}
 ENGINES = ("dma", "pe", "act", "dve")
 
 
@@ -58,6 +56,11 @@ def plan(records, slots):
             ready = []
             for r in mine:
                 t = 0.0
+                for n in r["after"]:
+                    if n not in done:
+                        t = None
+                if t is None:
+                    continue
                 for n in r["needs"]:
                     if n not in done:
                         t = None
@@ -112,9 +115,9 @@ def tile_infoncemi_pa_kernel(
     records = []
     emitters = {}
 
-    def op(name, engine, cycles, rank, needs, tiles, emit, lag=0):
+    def op(name, engine, cycles, rank, needs, tiles, emit, after=()):
         records.append({"name": name, "engine": engine, "cycles": cycles, "rank": rank, "needs": needs,
-                        "tiles": tiles, "lag": lag})
+                        "tiles": tiles, "lag": RESULT_LAG[engine], "after": after})
         emitters[name] = emit
 
     tau = {}
@@ -150,10 +153,6 @@ def tile_infoncemi_pa_kernel(
         nc.scalar.activation(out=warm2[:], in_=warm[:], func=ACT.Tanh)
         btile = const.tile([P, P], BF16)
         nc.vector.memset(btile[:], 0.0)
-        nc.scalar.dma_start(out=btile[0:16, :], in_=mu_b1.rearrange("(r p) -> r p", p=P))
-        nc.scalar.dma_start(out=btile[16:32, :], in_=lv_b1.rearrange("(r p) -> r p", p=P))
-        nc.scalar.dma_start(out=btile[32:36, :], in_=mu_b2.rearrange("(r p) -> r p", p=P))
-        nc.scalar.dma_start(out=btile[36:40, :], in_=lv_b2.rearrange("(r p) -> r p", p=P))
         ident_f = const.tile([P, P], F32)
         make_identity(nc, ident_f[:])
         ident_bf = const.tile([P, P], BF16)
@@ -199,6 +198,22 @@ def tile_infoncemi_pa_kernel(
         def quantise(codes, plane, grouped):
             nc.vector.quantize_mx(out=codes.bitcast(FP8X4), scales=plane, in_=grouped)
 
+        def bias_load():
+            nc.sync.dma_start(out=btile[0:16, :], in_=mu_b1.rearrange("(r p) -> r p", p=P))
+            nc.sync.dma_start(out=btile[16:32, :], in_=lv_b1.rearrange("(r p) -> r p", p=P))
+            nc.sync.dma_start(out=btile[32:36, :], in_=mu_b2.rearrange("(r p) -> r p", p=P))
+            nc.sync.dma_start(out=btile[36:40, :], in_=lv_b2.rearrange("(r p) -> r p", p=P))
+
+        def bias_transpose():
+            nc.tensor.transpose(rot("bias_t", "red", [P, P], BF16)[:], btile[:], ident_bf[:])
+
+        def bias_copy():
+            nc.vector.tensor_copy(out=bias_sb[:], in_=real["bias_t"][:, 0:40])
+
+        op("ld:bias", "dma", 200, 0, [], [], bias_load)
+        op("bt", "pe", 80, RANK["bias"], ["ld:bias"], [("bias_t", "red")], bias_transpose)
+        op("bc", "dve", 70, RANK["bias"], ["bt"], [("bias_t", "red")], bias_copy)
+
         XRAW = ("x_raw", "big")
         XG = ("x_grouped", "big")
         YRAW = ("y_raw", "big")
@@ -239,15 +254,15 @@ def tile_infoncemi_pa_kernel(
 
         for half in range(2):
             rank = -10.0 if half == 0 else RANK["x1"]
-            op("ld:x%d" % half, "dma", 1300, 0, [], [XRAW], lambda half=half: load_rows("x_raw", x_samples, half), 2300)
+            op("ld:x%d" % half, "dma", 1300, 0, [], [XRAW], lambda half=half: load_rows("x_raw", x_samples, half))
             for pair in range(2):
                 bank = ("xt%d%d" % (half, pair), "l1")
                 op("xt:%d:%d" % (half, pair), "pe", 312, rank, ["ld:x%d" % half], [XRAW, bank],
-                   lambda half=half, pair=pair: x_transposes(half, pair), 120)
+                   lambda half=half, pair=pair: x_transposes(half, pair))
                 op("xc:%d:%d" % (half, pair), "act", 522, rank, ["xt:%d:%d" % (half, pair)], [bank, XG],
                    lambda half=half, pair=pair: x_copy(half, pair))
             op("xq:%d" % half, "dve", 526, rank, ["xc:%d:0" % half, "xc:%d:1" % half], [XG],
-               lambda half=half: x_quantise(half), 240)
+               lambda half=half: x_quantise(half))
 
         def y_transposes(dt):
             yps = rot("yps%d" % dt, "l2", [P, 1024], BF16)
@@ -272,15 +287,15 @@ def tile_infoncemi_pa_kernel(
             nc.vector.tensor_scalar(out=vn[:], in0=vsum[:], scalar1=1.0 / NS, scalar2=None, op0=ALU.mult)
 
         for half in range(2):
-            op("ld:y%d" % half, "dma", 1300, 0, [], [YRAW], lambda half=half: load_rows("y_raw", y_samples, half), 2300)
+            op("ld:y%d" % half, "dma", 1300, 0, [], [YRAW], lambda half=half: load_rows("y_raw", y_samples, half))
         for dt in range(4):
             bank = ("yps%d" % dt, "l2")
             op("yt:%d" % dt, "pe", 500, RANK["y"] + dt * RANK["y_step"], ["ld:y0", "ld:y1"], [YRAW, bank],
-               lambda dt=dt: y_transposes(dt), 120)
+               lambda dt=dt: y_transposes(dt))
             op("yc:%d" % dt, "act", 1060, RANK["y"] + dt * RANK["y_step"], ["yt:%d" % dt], [bank],
                lambda dt=dt: y_copy(dt))
             op("ys:%d" % dt, "act", 1060, RANK["ys"] + dt * RANK["y_step"], ["ycn"], [], lambda dt=dt: y_spread(dt))
-        op("ycn", "dve", 140, RANK["y"] + 4 * RANK["y_step"], ["yc:%d" % dt for dt in range(4)], [], y_centre)
+        op("ycn", "dve", 140, RANK["y"] + 4 * RANK["y_step"], ["bc"] + ["yc:%d" % dt for dt in range(4)], [], y_centre)
         op("yv", "dve", 70, RANK["ys"] + 4 * RANK["y_step"], ["ys:%d" % dt for dt in range(4)], [], y_variance)
 
         def w_name(layer, head, g):
@@ -312,17 +327,17 @@ def tile_infoncemi_pa_kernel(
             quantise(wc[(layer, head)][:, sl], ws[(layer, head)][:, sl], real["grp" + w_name(layer, head, g)][:])
 
         chunks = sorted([(w_rank(layer, head, g), layer, head, g) for layer in (1, 2) for head in (MU, LV) for g in range(4)])
-        first_loads = ["ld:x0", "ld:w" + w_name(*chunks[0][1:]), "ld:x1", "ld:w" + w_name(*chunks[1][1:]), "ld:y0", "ld:y1"]
+        first_loads = ["ld:bias", "ld:x0", "ld:w" + w_name(*chunks[0][1:]), "ld:x1", "ld:w" + w_name(*chunks[1][1:]), "ld:y0", "ld:y1"]
         for rank, layer, head, g in chunks:
             n = w_name(layer, head, g)
             on_act = (layer, head, g) in SCALAR_REGROUP
             raw = ("raw" + n, "wraw")
             grp = ("grp" + n, "grps" if on_act else "grpv")
-            op("ld:w" + n, "dma", 1300, 0, [], [raw], lambda layer=layer, head=head, g=g: w_load(layer, head, g), 2300)
+            op("ld:w" + n, "dma", 1300, 0, [], [raw], lambda layer=layer, head=head, g=g: w_load(layer, head, g))
             op("wr:" + n, "act" if on_act else "dve", 2058 if on_act else 1042, rank, ["ld:w" + n], [raw, grp],
                lambda layer=layer, head=head, g=g, e=("act" if on_act else "dve"), tag=grp[1]: w_regroup(layer, head, g, e, tag))
             op("wq:" + n, "dve", 526, rank, ["wr:" + n], [grp],
-               lambda layer=layer, head=head, g=g: w_quantise(layer, head, g), 240)
+               lambda layer=layer, head=head, g=g: w_quantise(layer, head, g))
 
         def l1_pass(b, head, g, t):
             w = BLOCKS[b]
@@ -357,17 +372,16 @@ def tile_infoncemi_pa_kernel(
             for t in range(4):
                 bank = ("a%s%d" % (u, t), "l1")
                 needs = ["wq:" + w_name(1, head, g), "xq:%d" % (1 if OFFSETS[b] >= 512 else 0)]
-                if previous is not None:
-                    needs.append(previous)
+                behind = [previous] if previous is not None else []
                 previous = "l1:%s:%d" % (u, t)
                 op(previous, "pe", max(w / 2.0 + 8, 74), tau[(b, head, g)] + 0.01 * t, needs, [bank],
-                   lambda b=b, head=head, g=g, t=t: l1_pass(b, head, g, t), 200)
-                op("ex:%s:%d" % (u, t), "act", w + 10, tau[(b, head, g)] + 0.01 * t, [previous], [bank, hpl],
+                   lambda b=b, head=head, g=g, t=t: l1_pass(b, head, g, t), behind)
+                op("ex:%s:%d" % (u, t), "act", w + 10, tau[(b, head, g)] + 0.01 * t, [previous, "bc"], [bank, hpl],
                    lambda b=b, head=head, g=g, t=t: l1_exit(b, head, g, t))
             op("hr:" + u, "dve", 2 * w + 18, tau[(b, head, g)] + RANK["h"], ["ex:%s:%d" % (u, t) for t in range(4)], [hpl, hg],
                lambda b=b, head=head, g=g: h_regroup(b, head, g))
             op("hq:" + u, "dve", w + 14, tau[(b, head, g)] + RANK["h"], ["hr:" + u], [hg],
-               lambda b=b, head=head, g=g: h_quantise(b, head, g), 240)
+               lambda b=b, head=head, g=g: h_quantise(b, head, g))
 
         def l2_pass(head, b, dt, g):
             w = BLOCKS[b]
@@ -382,7 +396,7 @@ def tile_infoncemi_pa_kernel(
             w = BLOCKS[b]
             if b == 0:
                 return rot("kept%s0" % kind, "big", [P, 2048], F32, 64)[:, dt * w : (dt + 1) * w]
-            base = 0 if kind == "e" else 1024
+            base = 0 if kind == "e" else 4 * w
             return rot("kept%d" % b, "big", [P, 2048], F32, 64)[:, base + dt * w : base + (dt + 1) * w]
 
         def kept_key(kind, b):
@@ -444,12 +458,11 @@ def tile_infoncemi_pa_kernel(
                     bank = ("o%d%d%d" % (head, b, dt), "l2")
                     for g in range(4):
                         needs = ["wq:" + w_name(2, head, g), "hq:%d%d%d" % (b, head, g)]
-                        if g > 0:
-                            needs.append("l2:%d%d%d:%d" % (head, b, dt, g - 1))
-                        elif (head, b) not in OPEN_EARLY:
+                        behind = ["l2:%d%d%d:%d" % (head, b, dt, g - 1)] if g > 0 else []
+                        if g == 0 and (head, b) not in OPEN_EARLY:
                             needs.extend(["wq:" + w_name(2, head, 3), "hq:%d%d%d" % (b, head, 3)])
                         op("l2:%d%d%d:%d" % (head, b, dt, g), "pe", max(w / 2.0 + 8, 74), after(head, b) + RANK["l2"] + dt * step,
-                           needs, [bank], lambda head=head, b=b, dt=dt, g=g: l2_pass(head, b, dt, g), 200)
+                           needs, [bank], lambda head=head, b=b, dt=dt, g=g: l2_pass(head, b, dt, g), behind)
                 n = "%d%d" % (b, dt)
                 mbank = ("o%d%d%d" % (MU, b, dt), "l2")
                 lbank = ("o%d%d%d" % (LV, b, dt), "l2")
@@ -476,22 +489,22 @@ def tile_infoncemi_pa_kernel(
                     first = which == 1 and dt == (1 if PAIR_ADD[b] else 0)
                     last = which == 2 and dt == 3
                     if not PAIR_ADD[b]:
-                        op("r%d:%s" % (which, n), "pe", 2 * w, rrank, ["p%d:%s" % (which, n)] + reduces[-1:], [pk, red],
+                        op("r%d:%s" % (which, n), "pe", 2 * w, rrank, ["p%d:%s" % (which, n)], [pk, red],
                            lambda which=which, b=b, dt=dt, first=first, last=last: reduce_d(
-                               which, b, dt, "p%d%d%d" % (which, b, dt), first, last), 200)
+                               which, b, dt, "p%d%d%d" % (which, b, dt), first, last), reduces[-1:])
                         reduces.append("r%d:%s" % (which, n))
                     elif dt % 2 == 1:
                         sk = ("s%d%s" % (which, n), "s%d" % which)
                         op("a%d:%s" % (which, n), "dve", w + 15, rank, ["p%d:%s" % (which, n), "p%d:%d%d" % (which, b, dt - 1)],
                            [pk, ("p%d%d%d" % (which, b, dt - 1), "p%d" % which), sk],
                            lambda which=which, b=b, dt=dt: pair_sum(which, b, dt))
-                        op("r%d:%s" % (which, n), "pe", 2 * w, rrank, ["a%d:%s" % (which, n)] + reduces[-1:], [sk, red],
+                        op("r%d:%s" % (which, n), "pe", 2 * w, rrank, ["a%d:%s" % (which, n)], [sk, red],
                            lambda which=which, b=b, dt=dt, first=first, last=last: reduce_d(
-                               which, b, dt, "s%d%d%d" % (which, b, dt), first, last), 200)
+                               which, b, dt, "s%d%d%d" % (which, b, dt), first, last), reduces[-1:])
                         reduces.append("r%d:%s" % (which, n))
             rank = after(LV, b) + RANK["r"] + 4 * step
             op("res:%d" % b, "act", w + 10, rank, reduces[-1:], [red, ("res%d" % b, "res")], lambda b=b: result(b))
-            op("st:%d" % b, "dma", 20, rank, ["res:%d" % b], [("res%d" % b, "res")], lambda b=b: store(b), 2300)
+            op("st:%d" % b, "dma", 20, rank, ["res:%d" % b], [("res%d" % b, "res")], lambda b=b: store(b))
 
         loads = [r for r in records if r["engine"] == "dma"]
         rest = [r for r in records if r["engine"] != "dma"]
@@ -500,8 +513,5 @@ def tile_infoncemi_pa_kernel(
         order = plan(head_loads + tail_loads + rest, SLOTS)
 
         with tc.manual_schedule():
-            bt_ps = pools["red"].tile([P, P], BF16, tag="red", name="bias_t")
-            nc.tensor.transpose(bt_ps[:], btile[:], ident_bf[:])
-            nc.vector.tensor_copy(out=bias_sb[:], in_=bt_ps[:, 0:40])
             for start, name in order:
                 emitters[name]()

@@ -25,10 +25,12 @@ SCALAR_REGROUP = ((2, MU, 1), (2, MU, 3))
 PAIR_ADD = (True, True, True)
 OPEN_EARLY = ((LV, 2),)
 
-RANK = {"bias": -5, "x1": -2, "y": 1, "y_step": -2, "ys": 11, "w1": 3.5, "w2mu": 4.5, "w2lv": 11.1, "w2_step": 0.5, "h": 5.5, "l2": 3, "d_step": 1.8, "mu": 5.2, "lv": 3.7, "p": 1.9, "r": 3}
+RANK = {"ysum": 1.0, "bias": -5,"x1":-2,"y":1,"y_step":-2,"ys":11,"w1":3.5,"w2mu":4.5,"w2lv":11.1,"w2_step":0.5,"h":5.5,"d_step":1.8,"l2_00":3,"l2_10":3,"mu0":5.2,"lv0":3.7,"p0":1.9,"r0":3,"l2_01":3,"l2_11":3,"mu1":5.2,"lv1":3.7,"p1":1.9,"r1":3,"l2_02":3,"l2_12":3,"mu2":5.2,"lv2":3.7,"p2":1.9,"r2":3}
 SLOTS = {"wraw": 5, "grpv": 3, "grps": 1, "hpl": 4, "hg": 3, "l1": 4, "l2": 3, "red": 1, "big": 3,
          "dlt": 2, "th": 2, "wgt": 3, "p1": 3, "p2": 3, "s1": 2, "s2": 2, "res": 2}
+FIRST_LOADS = ("bias", "x0", 0, "x1", 1, "y0", "y1")
 HANDOVER = 320
+Y_COPY_CYCLES = 540
 RESULT_LAG = {"dma": 2300, "pe": 200, "act": 240, "dve": 240}
 ENGINES = ("dma", "pe", "act", "dve")
 
@@ -164,7 +166,8 @@ def tile_infoncemi_pa_kernel(
             nc.vector.memset(s[:, which : which + 1], value)
             sel.append(s)
         bias_sb = const.tile([P, 40], F32)
-        sy = const.tile([P, 4], F32)
+        ones_bf = const.tile([P, 32], BF16)
+        nc.vector.memset(ones_bf[:], 1.0)
         negc = const.tile([P, 4], F32)
         ebias = const.tile([P, 4], F32)
         vsum = const.tile([P, 4], F32)
@@ -272,11 +275,20 @@ def tile_infoncemi_pa_kernel(
                 )
 
         def y_copy(dt):
-            nc.scalar.activation(out=y_t[:, dt * 1024 : (dt + 1) * 1024], in_=real["yps%d" % dt][:], func=ACT.Copy,
-                                 accum_out=sy[:, dt : dt + 1])
+            nc.scalar.copy(out=y_t[:, dt * 1024 : (dt + 1) * 1024], in_=real["yps%d" % dt][:])
+
+        def y_sums():
+            sums = rot("y_sums", "red", [P, 4 * 32], F32)
+            for dt in range(4):
+                for r in range(8):
+                    nc.tensor.matmul(out=sums[:, dt * 32 : (dt + 1) * 32],
+                                     lhsT=big("y_raw")[:, r * 512 + dt * P : r * 512 + (dt + 1) * P], rhs=ones_bf[:],
+                                     start=(r == 0), stop=(r == 7))
 
         def y_centre():
-            nc.vector.tensor_scalar(out=negc[:], in0=sy[:], scalar1=-1.0 / NS, scalar2=None, op0=ALU.mult)
+            nc.vector.tensor_scalar(out=negc[:].rearrange("p (d o) -> p d o", o=1),
+                                    in0=real["y_sums"][:].rearrange("p (d c) -> p d c", c=32)[:, :, 0:1],
+                                    scalar1=-1.0 / NS, scalar2=None, op0=ALU.mult)
             nc.vector.tensor_tensor(out=ebias[:], in0=bias_sb[:, 32:36], in1=negc[:], op=ALU.add)
 
         def y_spread(dt):
@@ -292,10 +304,11 @@ def tile_infoncemi_pa_kernel(
             bank = ("yps%d" % dt, "l2")
             op("yt:%d" % dt, "pe", 500, RANK["y"] + dt * RANK["y_step"], ["ld:y0", "ld:y1"], [YRAW, bank],
                lambda dt=dt: y_transposes(dt))
-            op("yc:%d" % dt, "act", 1060, RANK["y"] + dt * RANK["y_step"], ["yt:%d" % dt], [bank],
+            op("yc:%d" % dt, "act", Y_COPY_CYCLES, RANK["y"] + dt * RANK["y_step"], ["yt:%d" % dt], [bank],
                lambda dt=dt: y_copy(dt))
-            op("ys:%d" % dt, "act", 1060, RANK["ys"] + dt * RANK["y_step"], ["ycn"], [], lambda dt=dt: y_spread(dt))
-        op("ycn", "dve", 140, RANK["y"] + 4 * RANK["y_step"], ["bc"] + ["yc:%d" % dt for dt in range(4)], [], y_centre)
+            op("ys:%d" % dt, "act", 1060, RANK["ys"] + dt * RANK["y_step"], ["ycn", "yc:%d" % dt], [], lambda dt=dt: y_spread(dt))
+        op("ysum", "pe", 32 * 70, RANK["ysum"], ["ld:y0", "ld:y1"], [YRAW, ("y_sums", "red")], y_sums)
+        op("ycn", "dve", 140, RANK["ysum"], ["bc", "ysum"], [("y_sums", "red")], y_centre)
         op("yv", "dve", 70, RANK["ys"] + 4 * RANK["y_step"], ["ys:%d" % dt for dt in range(4)], [], y_variance)
 
         def w_name(layer, head, g):
@@ -327,7 +340,7 @@ def tile_infoncemi_pa_kernel(
             quantise(wc[(layer, head)][:, sl], ws[(layer, head)][:, sl], real["grp" + w_name(layer, head, g)][:])
 
         chunks = sorted([(w_rank(layer, head, g), layer, head, g) for layer in (1, 2) for head in (MU, LV) for g in range(4)])
-        first_loads = ["ld:bias", "ld:x0", "ld:w" + w_name(*chunks[0][1:]), "ld:x1", "ld:w" + w_name(*chunks[1][1:]), "ld:y0", "ld:y1"]
+        first_loads = ["ld:w" + w_name(*chunks[item][1:]) if isinstance(item, int) else "ld:" + item for item in FIRST_LOADS]
         for rank, layer, head, g in chunks:
             n = w_name(layer, head, g)
             on_act = (layer, head, g) in SCALAR_REGROUP
@@ -461,31 +474,31 @@ def tile_infoncemi_pa_kernel(
                         behind = ["l2:%d%d%d:%d" % (head, b, dt, g - 1)] if g > 0 else []
                         if g == 0 and (head, b) not in OPEN_EARLY:
                             needs.extend(["wq:" + w_name(2, head, 3), "hq:%d%d%d" % (b, head, 3)])
-                        op("l2:%d%d%d:%d" % (head, b, dt, g), "pe", max(w / 2.0 + 8, 74), after(head, b) + RANK["l2"] + dt * step,
+                        op("l2:%d%d%d:%d" % (head, b, dt, g), "pe", max(w / 2.0 + 8, 74), after(head, b) + RANK["l2_%d%d" % (head, b)] + dt * step,
                            needs, [bank], lambda head=head, b=b, dt=dt, g=g: l2_pass(head, b, dt, g), behind)
                 n = "%d%d" % (b, dt)
                 mbank = ("o%d%d%d" % (MU, b, dt), "l2")
                 lbank = ("o%d%d%d" % (LV, b, dt), "l2")
-                rank = after(MU, b) + RANK["mu"] + dt * step
+                rank = after(MU, b) + RANK["mu%d" % b] + dt * step
                 op("md:" + n, "dve", w + 15, rank, ["l2:%d%d%d:3" % (MU, b, dt), "yc:%d" % dt], [mbank, ("dlt" + n, "dlt")],
                    lambda b=b, dt=dt: mu_delta(b, dt))
                 op("me:" + n, "act", w + 10, rank, ["l2:%d%d%d:3" % (MU, b, dt), "ycn"], [mbank, kept_key("e", b)],
                    lambda b=b, dt=dt: mu_centred_square(b, dt))
                 op("ms:" + n, "act", w + 10, rank, ["md:" + n], [("dlt" + n, "dlt"), kept_key("s", b)],
                    lambda b=b, dt=dt: mu_delta_square(b, dt))
-                rank = after(LV, b) + RANK["lv"] + dt * step
+                rank = after(LV, b) + RANK["lv%d" % b] + dt * step
                 op("lt:" + n, "act", w + 10, rank, ["l2:%d%d%d:3" % (LV, b, dt)], [lbank, ("th" + n, "th")],
                    lambda b=b, dt=dt: lv_tanh(b, dt))
                 op("lx:" + n, "act", w + 10, rank, ["lt:" + n], [("th" + n, "th"), ("wgt" + n, "wgt")],
                    lambda b=b, dt=dt: lv_exp(b, dt))
                 for which in (1, 2):
-                    rank = after(LV, b) + RANK["p"] + dt * step
+                    rank = after(LV, b) + RANK["p%d" % b] + dt * step
                     pk = ("p%d%s" % (which, n), "p%d" % which)
                     needs = ["lx:" + n, "ms:" + n] if which == 1 else ["lx:" + n, "me:" + n, "yv"]
                     op("p%d:%s" % (which, n), "dve", w + 15, rank, needs,
                        [pk, ("wgt" + n, "wgt"), kept_key("s" if which == 1 else "e", b)],
                        lambda which=which, b=b, dt=dt: product(which, b, dt))
-                    rrank = after(LV, b) + RANK["r"] + dt * step
+                    rrank = after(LV, b) + RANK["r%d" % b] + dt * step
                     first = which == 1 and dt == (1 if PAIR_ADD[b] else 0)
                     last = which == 2 and dt == 3
                     if not PAIR_ADD[b]:
@@ -502,7 +515,7 @@ def tile_infoncemi_pa_kernel(
                            lambda which=which, b=b, dt=dt, first=first, last=last: reduce_d(
                                which, b, dt, "s%d%d%d" % (which, b, dt), first, last), reduces[-1:])
                         reduces.append("r%d:%s" % (which, n))
-            rank = after(LV, b) + RANK["r"] + 4 * step
+            rank = after(LV, b) + RANK["r%d" % b] + 4 * step
             op("res:%d" % b, "act", w + 10, rank, reduces[-1:], [red, ("res%d" % b, "res")], lambda b=b: result(b))
             op("st:%d" % b, "dma", 20, rank, ["res:%d" % b], [("res%d" % b, "res")], lambda b=b: store(b))
 

@@ -25,12 +25,12 @@ SCALAR_REGROUP = ((2, MU, 1), (2, MU, 3))
 PAIR_ADD = (True, True, True)
 OPEN_EARLY = ((LV, 2),)
 
-RANK = {"ysum": 1.0, "bias": -5,"x1":-2,"y":1,"y_step":-2,"ys":11,"w1":3.5,"w2mu":4.5,"w2lv":11.1,"w2_step":0.5,"h":5.5,"d_step":1.8,"l2_00":3,"l2_10":3,"mu0":5.2,"lv0":3.7,"p0":1.9,"r0":3,"l2_01":3,"l2_11":3,"mu1":5.2,"lv1":3.7,"p1":1.9,"r1":3,"l2_02":3,"l2_12":3,"mu2":5.2,"lv2":3.7,"p2":1.9,"r2":3}
-SLOTS = {"wraw": 5, "grpv": 3, "grps": 1, "hpl": 4, "hg": 3, "l1": 4, "l2": 3, "red": 1, "big": 3,
+RANK = {"bias": -5, "x1": -2, "y": 1, "y_step": -2, "ys": 15.5, "w1": 3.5, "w2mu": 5.0, "w2lv": 11.1, "w2_step": 0.5, "h": 5.5, "d_step": 1.8, "l2_00": 4, "l2_10": 3, "mu0": 5.2, "lv0": 3.7, "p0": 1.9, "r0": 4, "l2_01": 3, "l2_11": 3.0, "mu1": 5.2, "lv1": 3.7, "p1": 1.9, "r1": 7.5, "l2_02": 1, "l2_12": 3, "mu2": 6.2, "lv2": 3.7, "p2": 1.9, "r2": 3}
+SLOTS = {"wraw": 5, "grpv": 3, "grps": 1, "hpl": 5, "hg": 3, "l1": 4, "l2": 3, "red": 1, "big": 3,
          "dlt": 2, "th": 2, "wgt": 3, "p1": 3, "p2": 3, "s1": 2, "s2": 2, "res": 2}
 FIRST_LOADS = ("bias", "x0", 0, "x1", 1, "y0", "y1")
 HANDOVER = 320
-Y_COPY_CYCLES = 540
+DMA_CYCLES = 1300
 RESULT_LAG = {"dma": 2300, "pe": 200, "act": 240, "dve": 240}
 ENGINES = ("dma", "pe", "act", "dve")
 
@@ -166,8 +166,7 @@ def tile_infoncemi_pa_kernel(
             nc.vector.memset(s[:, which : which + 1], value)
             sel.append(s)
         bias_sb = const.tile([P, 40], F32)
-        ones_bf = const.tile([P, 32], BF16)
-        nc.vector.memset(ones_bf[:], 1.0)
+        sy = const.tile([P, 4], F32)
         negc = const.tile([P, 4], F32)
         ebias = const.tile([P, 4], F32)
         vsum = const.tile([P, 4], F32)
@@ -257,7 +256,7 @@ def tile_infoncemi_pa_kernel(
 
         for half in range(2):
             rank = -10.0 if half == 0 else RANK["x1"]
-            op("ld:x%d" % half, "dma", 1300, 0, [], [XRAW], lambda half=half: load_rows("x_raw", x_samples, half))
+            op("ld:x%d" % half, "dma", DMA_CYCLES, 0, [], [XRAW], lambda half=half: load_rows("x_raw", x_samples, half))
             for pair in range(2):
                 bank = ("xt%d%d" % (half, pair), "l1")
                 op("xt:%d:%d" % (half, pair), "pe", 312, rank, ["ld:x%d" % half], [XRAW, bank],
@@ -275,20 +274,11 @@ def tile_infoncemi_pa_kernel(
                 )
 
         def y_copy(dt):
-            nc.scalar.copy(out=y_t[:, dt * 1024 : (dt + 1) * 1024], in_=real["yps%d" % dt][:])
-
-        def y_sums():
-            sums = rot("y_sums", "red", [P, 4 * 32], F32)
-            for dt in range(4):
-                for r in range(8):
-                    nc.tensor.matmul(out=sums[:, dt * 32 : (dt + 1) * 32],
-                                     lhsT=big("y_raw")[:, r * 512 + dt * P : r * 512 + (dt + 1) * P], rhs=ones_bf[:],
-                                     start=(r == 0), stop=(r == 7))
+            nc.scalar.activation(out=y_t[:, dt * 1024 : (dt + 1) * 1024], in_=real["yps%d" % dt][:], func=ACT.Copy,
+                                 accum_out=sy[:, dt : dt + 1])
 
         def y_centre():
-            nc.vector.tensor_scalar(out=negc[:].rearrange("p (d o) -> p d o", o=1),
-                                    in0=real["y_sums"][:].rearrange("p (d c) -> p d c", c=32)[:, :, 0:1],
-                                    scalar1=-1.0 / NS, scalar2=None, op0=ALU.mult)
+            nc.vector.tensor_scalar(out=negc[:], in0=sy[:], scalar1=-1.0 / NS, scalar2=None, op0=ALU.mult)
             nc.vector.tensor_tensor(out=ebias[:], in0=bias_sb[:, 32:36], in1=negc[:], op=ALU.add)
 
         def y_spread(dt):
@@ -299,16 +289,15 @@ def tile_infoncemi_pa_kernel(
             nc.vector.tensor_scalar(out=vn[:], in0=vsum[:], scalar1=1.0 / NS, scalar2=None, op0=ALU.mult)
 
         for half in range(2):
-            op("ld:y%d" % half, "dma", 1300, 0, [], [YRAW], lambda half=half: load_rows("y_raw", y_samples, half))
+            op("ld:y%d" % half, "dma", DMA_CYCLES, 0, [], [YRAW], lambda half=half: load_rows("y_raw", y_samples, half))
         for dt in range(4):
             bank = ("yps%d" % dt, "l2")
             op("yt:%d" % dt, "pe", 500, RANK["y"] + dt * RANK["y_step"], ["ld:y0", "ld:y1"], [YRAW, bank],
                lambda dt=dt: y_transposes(dt))
-            op("yc:%d" % dt, "act", Y_COPY_CYCLES, RANK["y"] + dt * RANK["y_step"], ["yt:%d" % dt], [bank],
+            op("yc:%d" % dt, "act", 1060, RANK["y"] + dt * RANK["y_step"], ["yt:%d" % dt], [bank],
                lambda dt=dt: y_copy(dt))
-            op("ys:%d" % dt, "act", 1060, RANK["ys"] + dt * RANK["y_step"], ["ycn", "yc:%d" % dt], [], lambda dt=dt: y_spread(dt))
-        op("ysum", "pe", 32 * 70, RANK["ysum"], ["ld:y0", "ld:y1"], [YRAW, ("y_sums", "red")], y_sums)
-        op("ycn", "dve", 140, RANK["ysum"], ["bc", "ysum"], [("y_sums", "red")], y_centre)
+            op("ys:%d" % dt, "act", 1060, RANK["ys"] + dt * RANK["y_step"], ["ycn"], [], lambda dt=dt: y_spread(dt))
+        op("ycn", "dve", 140, RANK["y"] + 4 * RANK["y_step"], ["bc"] + ["yc:%d" % dt for dt in range(4)], [], y_centre)
         op("yv", "dve", 70, RANK["ys"] + 4 * RANK["y_step"], ["ys:%d" % dt for dt in range(4)], [], y_variance)
 
         def w_name(layer, head, g):
@@ -346,7 +335,7 @@ def tile_infoncemi_pa_kernel(
             on_act = (layer, head, g) in SCALAR_REGROUP
             raw = ("raw" + n, "wraw")
             grp = ("grp" + n, "grps" if on_act else "grpv")
-            op("ld:w" + n, "dma", 1300, 0, [], [raw], lambda layer=layer, head=head, g=g: w_load(layer, head, g))
+            op("ld:w" + n, "dma", DMA_CYCLES, 0, [], [raw], lambda layer=layer, head=head, g=g: w_load(layer, head, g))
             op("wr:" + n, "act" if on_act else "dve", 2058 if on_act else 1042, rank, ["ld:w" + n], [raw, grp],
                lambda layer=layer, head=head, g=g, e=("act" if on_act else "dve"), tag=grp[1]: w_regroup(layer, head, g, e, tag))
             op("wq:" + n, "dve", 526, rank, ["wr:" + n], [grp],

@@ -18,94 +18,30 @@ NS = 1024
 MU = 0
 LV = 1
 
-BLOCKS = (512, 256, 256)
-OFFSETS = tuple(sum(BLOCKS[:b]) for b in range(len(BLOCKS)))
-UNITS = [(b, head, g) for b in range(len(BLOCKS)) for head in (MU, LV) for g in range(4)]
-SCALAR_REGROUP = ((2, MU, 1), (2, MU, 3))
-PAIR_ADD = (True, True, True)
-OPEN_EARLY = ((LV, 2),)
+SLOTS = {"xbig": 1, "wraw": 5, "wraws": 2, "grp": 3, "hpl": 4, "hg": 3, "l1": 4, "l2": 3, "red": 1,
+         "dlt": 3, "th": 2, "wgt": 4, "p1": 3, "p2": 3}
 
-RANK = {"bias": -5, "x1": -2, "y": 1, "y_step": -2, "ys": 15.5, "w1": 3.5, "w2mu": 5.0, "w2lv": 11.1, "w2_step": 0.5, "h": 5.5, "d_step": 1.8, "l2_00": 4, "l2_10": 3, "mu0": 5.2, "lv0": 3.7, "p0": 1.9, "r0": 4, "l2_01": 3, "l2_11": 3.0, "mu1": 5.2, "lv1": 3.7, "p1": 1.9, "r1": 7.5, "l2_02": 1, "l2_12": 3, "mu2": 6.2, "lv2": 3.7, "p2": 1.9, "r2": 3}
-SLOTS = {"wraw": 5, "grpv": 3, "grps": 1, "hpl": 5, "hg": 3, "l1": 4, "l2": 3, "red": 1, "big": 3,
-         "dlt": 2, "th": 2, "wgt": 3, "p1": 3, "p2": 3, "s1": 2, "s2": 2, "res": 2}
-FIRST_LOADS = ("bias", "x0", 0, "x1", 1, "y0", "y1")
-HANDOVER = 320
-DMA_CYCLES = 1300
-RESULT_LAG = {"dma": 2300, "pe": 200, "act": 240, "dve": 240}
-ENGINES = ("dma", "pe", "act", "dve")
-
-
-def plan(records, slots):
-    users = {}
-    for r in records:
-        for key, tag in r["tiles"]:
-            users[key] = users.get(key, 0) + 1
-    done = {}
-    engine_of = {}
-    free_at = {}
-    taken = {}
-    released = {}
-    touched = {}
-    placed = set()
-    todo = list(records)
-    order = []
-    while todo:
-        best = None
-        for engine in ENGINES:
-            mine = [r for r in todo if r["engine"] == engine]
-            if engine == "dma":
-                mine = mine[:1]
-            ready = []
-            for r in mine:
-                t = 0.0
-                for n in r["after"]:
-                    if n not in done:
-                        t = None
-                if t is None:
-                    continue
-                for n in r["needs"]:
-                    if n not in done:
-                        t = None
-                        break
-                    t = max(t, done[n] + (HANDOVER if engine_of[n] != engine else 0))
-                if t is None:
-                    continue
-                for key, tag in r["tiles"]:
-                    if key not in placed and taken.get(tag, 0) >= slots[tag]:
-                        if not released.get(tag):
-                            t = None
-                            break
-                        t = max(t, min(released[tag]) + HANDOVER)
-                if t is not None:
-                    ready.append((t, r))
-            if not ready:
-                continue
-            start = max(free_at.get(engine, 0.0), min(t for t, r in ready))
-            pick = min((r for t, r in ready if t <= start + 1e-9), key=lambda r: r["rank"])
-            if best is None or start < best[0]:
-                best = (start, pick)
-        assert best is not None, "the plan is stuck"
-        start, r = best
-        finish = start + r["cycles"]
-        free_at[r["engine"]] = finish
-        done[r["name"]] = finish + r["lag"]
-        engine_of[r["name"]] = r["engine"]
-        order.append((start, r["name"]))
-        todo = [q for q in todo if q["name"] != r["name"]]
-        for key, tag in r["tiles"]:
-            if key not in placed:
-                placed.add(key)
-                if taken.get(tag, 0) >= slots[tag]:
-                    first = min(released[tag])
-                    at = released[tag].index(first)
-                    released[tag] = released[tag][:at] + released[tag][at + 1 :]
-                else:
-                    taken[tag] = taken.get(tag, 0) + 1
-            users[key] = users[key] - 1
-            touched[key] = max(touched.get(key, 0.0), finish + r["lag"])
-            if users[key] == 0:
-                released[tag] = released.get(tag, []) + [touched[key]]
-    return order
+BLOCKS = ((0, 512), (512, 512), (512, 256), (768, 256))
+OF_HEAD = {MU: (0, 1), LV: (0, 2, 3)}
+ORDER = ((MU, 0), (LV, 0), (MU, 1), (LV, 2), (LV, 3))
+UNITS = [(head, g, b) for head, b in ORDER for g in range(4)]
+CHUNKS = [(1, MU, 0, 256), (1, MU, 256, 256)] + [(1, MU, s, 512) for s in (512, 1024, 1536)] + [
+    (layer, head, s, 512) for layer, head in ((1, LV), (2, MU), (2, LV)) for s in (0, 512, 1024, 1536)
+]
+ON_SCALAR = ((2, MU, 0, 512), (2, MU, 512, 512), (2, MU, 1024, 512))
+PAIRED = ((0, 3), (2, 1), (2, 3), (3, 1), (3, 3))
+LATE = ()
+HEAD = ("ld:x00", "ld:x01", "ld:100a", "ld:bias", "ld:100b", "xt:00", "xt:01", "xc:00", "xc:01", "bt", "wr:100a", "wq:100a", "bc", "xq:0", "wr:100b", "wq:100b", "l1:000:0", "l1:000:1", "l1:000:2", "l1:000:3")
+LOADS = ("x00", "x01", "100a", "bias", "100b", "101", "102", "103", "110", "111", "112", "113", "200", "x1", "201", "y0", "y1", "202", "203", "210", "211", "212", "213")
+X_RANK = (-10, 2)
+Y_RANK = 4
+W1_AHEAD = 3
+W2_RANK = {MU: 6, LV: 8}
+W2_STEP = {MU: 1, LV: 1}
+RA_AHEAD = 0
+H_BEHIND = 5
+STEP = 1
+BEHIND = {(MU, 0): 6, (MU, 1): 3, (LV, 0): 4, (LV, 2): 3, (LV, 3): 3}
 
 
 def tile_infoncemi_pa_kernel(
@@ -114,40 +50,29 @@ def tile_infoncemi_pa_kernel(
     nc = tc.nc
     w_dram = {(1, MU): mu_W1, (1, LV): lv_W1, (2, MU): mu_W2, (2, LV): lv_W2}
     outs = (out_0, out_1)
-    records = []
-    emitters = {}
+    jobs = {}
 
-    def op(name, engine, cycles, rank, needs, tiles, emit, after=()):
-        records.append({"name": name, "engine": engine, "cycles": cycles, "rank": rank, "needs": needs,
-                        "tiles": tiles, "lag": RESULT_LAG[engine], "after": after})
-        emitters[name] = emit
-
-    tau = {}
-    clock = 0.0
-    for b, head, g in UNITS:
-        tau[(b, head, g)] = clock
-        clock += BLOCKS[b] / 512.0
-
-    def after(head, b):
-        return tau[(b, head, 3)] + BLOCKS[b] / 512.0
+    def job(name, needs, tiles, emit):
+        jobs[name] = (needs, tiles, emit)
 
     with ExitStack() as ctx:
         const = ctx.enter_context(tc.tile_pool(name="const", bufs=1))
         keep = ctx.enter_context(tc.tile_pool(name="keep", bufs=1))
         pools = {}
-        for tag in ("wraw", "grpv", "grps", "hpl", "hg", "big", "dlt", "th", "wgt", "p1", "p2", "s1", "s2", "res"):
+        for tag in ("xbig", "wraw", "wraws", "grp", "hpl", "hg", "dlt", "th", "wgt", "p1", "p2"):
             pools[tag] = ctx.enter_context(tc.tile_pool(name="pool_" + tag, bufs=SLOTS[tag]))
         for tag in ("l1", "l2", "red"):
             pools[tag] = ctx.enter_context(tc.psum_pool(name="psum_" + tag, bufs=SLOTS[tag]))
         real = {}
 
-        def rot(key, tag, shape, dtype, align=None):
-            if key not in real:
+        def rot(key, shape, dtype, align=None):
+            name, tag = key
+            if name not in real:
                 if align is None:
-                    real[key] = pools[tag].tile(shape, dtype, tag=tag, name=key)
+                    real[name] = pools[tag].tile(shape, dtype, tag=tag, name=name)
                 else:
-                    real[key] = pools[tag].tile(shape, dtype, tag=tag, name=key, align_bytes=align)
-            return real[key]
+                    real[name] = pools[tag].tile(shape, dtype, tag=tag, name=name, align_bytes=align)
+            return real[name]
 
         warm = const.tile([P, 1], F32)
         nc.vector.memset(warm[:], 0.0)
@@ -165,17 +90,24 @@ def tile_infoncemi_pa_kernel(
             nc.vector.memset(s[:], 0.0)
             nc.vector.memset(s[:, which : which + 1], value)
             sel.append(s)
+        ones = const.tile([P, 2], BF16)
+        nc.vector.memset(ones[:], 1.0)
         bias_sb = const.tile([P, 40], F32)
-        sy = const.tile([P, 4], F32)
         negc = const.tile([P, 4], F32)
+        csq = const.tile([P, 4], F32)
         ebias = const.tile([P, 4], F32)
         vsum = const.tile([P, 4], F32)
         vn = const.tile([P, 4], F32)
-        junk = const.tile([P, 1024], BF16)
+        junk = const.tile([P, P], F32)
 
         xc = keep.tile([P, 1024], U32, align_bytes=64)
         xs = keep.tile([P, 1024], U8, align_bytes=64)
+        y_raw = keep.tile([P, 4096], BF16)
         y_t = keep.tile([P, 4096], BF16)
+        sq_d = keep.tile([P, 4096], F32)
+        res = {}
+        for b in OF_HEAD[LV]:
+            res[b] = keep.tile([P, BLOCKS[b][1]], F32, name="res%d" % b)
         wc = {}
         ws = {}
         hc = {}
@@ -185,17 +117,12 @@ def tile_infoncemi_pa_kernel(
                 wc[(layer, head)] = keep.tile([P, 2048], U32, align_bytes=64, name="wc%d%d" % (layer, head))
                 ws[(layer, head)] = keep.tile([P, 2048], U8, align_bytes=64, name="ws%d%d" % (layer, head))
         for head in (MU, LV):
-            for b in range(len(BLOCKS)):
-                hc[(head, b)] = keep.tile([P, 4 * BLOCKS[b]], U32, align_bytes=64, name="hc%d%d" % (head, b))
-                hs[(head, b)] = keep.tile([P, 4 * BLOCKS[b]], U8, align_bytes=64, name="hs%d%d" % (head, b))
+            for b in OF_HEAD[head]:
+                hc[(head, b)] = keep.tile([P, 4 * BLOCKS[b][1]], U32, align_bytes=64, name="hc%d%d" % (head, b))
+                hs[(head, b)] = keep.tile([P, 4 * BLOCKS[b][1]], U8, align_bytes=64, name="hs%d%d" % (head, b))
 
-        def regroup(engine, dst, src, width):
-            d = dst.rearrange("p (c i t) -> p c t i", i=4, t=4)
-            s = src.rearrange("p (t c i) -> p c t i", t=4, i=4)
-            if engine == "act":
-                nc.scalar.copy(out=d, in_=s)
-            else:
-                nc.vector.tensor_copy(out=d, in_=s)
+        def regroup(copy, dst, src):
+            copy(out=dst.rearrange("p (c i t) -> p c t i", i=4, t=4), in_=src.rearrange("p (t c i) -> p c t i", t=4, i=4))
 
         def quantise(codes, plane, grouped):
             nc.vector.quantize_mx(out=codes.bitcast(FP8X4), scales=plane, in_=grouped)
@@ -206,33 +133,58 @@ def tile_infoncemi_pa_kernel(
             nc.sync.dma_start(out=btile[32:36, :], in_=mu_b2.rearrange("(r p) -> r p", p=P))
             nc.sync.dma_start(out=btile[36:40, :], in_=lv_b2.rearrange("(r p) -> r p", p=P))
 
+        def load_rows(tile, src, r0, rows):
+            nc.sync.dma_start(
+                out=tile[:, r0 * 512 : (r0 + rows) * 512].rearrange("p (r k) -> p r k", r=rows),
+                in_=src[r0 * P : (r0 + rows) * P, :].rearrange("(r p) k -> p r k", p=P),
+            )
+
+        def x_all():
+            return rot(("x", "xbig"), [P, 8192], BF16, 64)
+
+        def sq_e():
+            return rot(("sq_e", "xbig"), [P, 4096], F32, 64)
+
+        def wname(c):
+            return "%d%d%d" % (c[0], c[1], c[2] // 512) + ("" if c[3] == 512 else "ab"[c[2] // 256])
+
+        def wkey(kind, c):
+            return (kind + wname(c), "wraws" if kind == "wraw" and c in ON_SCALAR else kind)
+
+        def w_load(c):
+            layer, head, s, w = c
+            raw = rot(wkey("wraw", c), [P, 4 * w], BF16)
+            r3 = raw[:].rearrange("p (t c) -> p t c", t=4)
+            if layer == 1:
+                src = w_dram[(1, head)].rearrange("(u q e) c -> u q e c", u=2, e=2)
+                for u in range(2):
+                    nc.sync.dma_start(out=r3[:, 2 * u : 2 * u + 2, :], in_=src[u, :, :, s : s + w])
+            else:
+                nc.sync.dma_start(
+                    out=r3, in_=w_dram[(2, head)][s : s + w, :].rearrange("(t p) d -> p t d", p=P)
+                )
+
+        job("ld:bias", [], [], bias_load)
+        for half in range(2):
+            job("ld:y%d" % half, [], [], lambda half=half: load_rows(y_raw, y_samples, 4 * half, 4))
+        for n, r0, rows in (("x00", 0, 2), ("x01", 2, 2), ("x1", 4, 4)):
+            job("ld:" + n, [], [("x", "xbig")], lambda r0=r0, rows=rows: load_rows(x_all(), x_samples, r0, rows))
+        for c in CHUNKS:
+            job("ld:" + wname(c), [], [wkey("wraw", c)], lambda c=c: w_load(c))
+
         def bias_transpose():
-            nc.tensor.transpose(rot("bias_t", "red", [P, P], BF16)[:], btile[:], ident_bf[:])
+            nc.tensor.transpose(rot(("bias_t", "red"), [P, P], BF16)[:], btile[:], ident_bf[:])
 
         def bias_copy():
             nc.vector.tensor_copy(out=bias_sb[:], in_=real["bias_t"][:, 0:40])
 
-        op("ld:bias", "dma", 200, 0, [], [], bias_load)
-        op("bt", "pe", 80, RANK["bias"], ["ld:bias"], [("bias_t", "red")], bias_transpose)
-        op("bc", "dve", 70, RANK["bias"], ["bt"], [("bias_t", "red")], bias_copy)
-
-        XRAW = ("x_raw", "big")
-        XG = ("x_grouped", "big")
-        YRAW = ("y_raw", "big")
-
-        def big(key):
-            return rot(key, "big", [P, 4096], BF16, 64)
-
-        def load_rows(key, src, half):
-            nc.sync.dma_start(
-                out=big(key)[:, half * 2048 : (half + 1) * 2048].rearrange("p (r k) -> p r k", r=4),
-                in_=src[half * 512 : (half + 1) * 512, :].rearrange("(r p) k -> p r k", p=P),
-            )
+        job("bt", ["ld:bias"], [("bias_t", "red")], bias_transpose)
+        job("bc", ["bt"], [("bias_t", "red")], bias_copy)
 
         def x_transposes(half, pair):
             r0 = half * 4 + pair * 2
-            xt = rot("xt%d%d" % (half, pair), "l1", [P, 512], F32)
-            words = big("x_raw")[:].bitcast(F32)
+            xt = rot(("xt%d%d" % (half, pair), "l1"), [P, 512], F32)
+            words = x_all()[:, 0:4096].bitcast(F32)
             for rr in range(2):
                 for u in range(2):
                     nc.tensor.transpose(
@@ -244,276 +196,320 @@ def tile_infoncemi_pa_kernel(
         def x_copy(half, pair):
             r0 = half * 4 + pair * 2
             nc.scalar.copy(
-                out=big("x_grouped")[:].bitcast(F32)[:, r0 * 256 : r0 * 256 + 512].rearrange(
-                    "p (r n u) -> p r n u", r=2, u=2
-                ),
+                out=x_all()[:, 4096:8192].bitcast(F32)[:, r0 * 256 : r0 * 256 + 512].rearrange("p (r n u) -> p r n u", r=2, u=2),
                 in_=real["xt%d%d" % (half, pair)][:].rearrange("p (r u n) -> p r n u", r=2, u=2),
             )
 
         def x_quantise(half):
             sl = slice(half * 512, (half + 1) * 512)
-            quantise(xc[:, sl], xs[:, sl], big("x_grouped")[:, half * 2048 : (half + 1) * 2048])
+            quantise(xc[:, sl], xs[:, sl], x_all()[:, 4096 + half * 2048 : 4096 + (half + 1) * 2048])
 
         for half in range(2):
-            rank = -10.0 if half == 0 else RANK["x1"]
-            op("ld:x%d" % half, "dma", DMA_CYCLES, 0, [], [XRAW], lambda half=half: load_rows("x_raw", x_samples, half))
             for pair in range(2):
                 bank = ("xt%d%d" % (half, pair), "l1")
-                op("xt:%d:%d" % (half, pair), "pe", 312, rank, ["ld:x%d" % half], [XRAW, bank],
-                   lambda half=half, pair=pair: x_transposes(half, pair))
-                op("xc:%d:%d" % (half, pair), "act", 522, rank, ["xt:%d:%d" % (half, pair)], [bank, XG],
-                   lambda half=half, pair=pair: x_copy(half, pair))
-            op("xq:%d" % half, "dve", 526, rank, ["xc:%d:0" % half, "xc:%d:1" % half], [XG],
-               lambda half=half: x_quantise(half))
+                job("xt:%d%d" % (half, pair), ["ld:x0%d" % pair if half == 0 else "ld:x1"], [bank, ("x", "xbig")], lambda half=half, pair=pair: x_transposes(half, pair))
+                job("xc:%d%d" % (half, pair), ["xt:%d%d" % (half, pair)], [bank, ("x", "xbig")], lambda half=half, pair=pair: x_copy(half, pair))
+            job("xq:%d" % half, ["xc:%d0" % half, "xc:%d1" % half], [("x", "xbig")], lambda half=half: x_quantise(half))
 
         def y_transposes(dt):
-            yps = rot("yps%d" % dt, "l2", [P, 1024], BF16)
+            yps = rot(("yps%d" % dt, "l2"), [P, 1024], BF16)
             for r in range(8):
                 nc.tensor.transpose(
-                    yps[:, r * P : (r + 1) * P], big("y_raw")[:, r * 512 + dt * P : r * 512 + (dt + 1) * P], ident_bf[:]
+                    yps[:, r * P : (r + 1) * P], y_raw[:, r * 512 + dt * P : r * 512 + (dt + 1) * P], ident_bf[:]
                 )
 
         def y_copy(dt):
-            nc.scalar.activation(out=y_t[:, dt * 1024 : (dt + 1) * 1024], in_=real["yps%d" % dt][:], func=ACT.Copy,
-                                 accum_out=sy[:, dt : dt + 1])
+            nc.scalar.copy(out=y_t[:, dt * 1024 : (dt + 1) * 1024], in_=real["yps%d" % dt][:])
+
+        def y_products():
+            prod = rot(("yprod", "l2"), [P, 512], F32)
+            for dt in range(4):
+                for r in range(8):
+                    sl = slice(r * 512 + dt * P, r * 512 + (dt + 1) * P)
+                    nc.tensor.matmul(out=prod[:, dt * P : (dt + 1) * P], lhsT=y_raw[:, sl], rhs=y_raw[:, sl],
+                                     start=(r == 0), stop=(r == 7))
+
+        def y_sums():
+            tot = rot(("ytot", "red"), [P, 8], F32)
+            for dt in range(4):
+                for r in range(8):
+                    sl = slice(r * 512 + dt * P, r * 512 + (dt + 1) * P)
+                    nc.tensor.matmul(out=tot[:, 2 * dt : 2 * dt + 2], lhsT=y_raw[:, sl], rhs=ones[:],
+                                     start=(r == 0), stop=(r == 7))
 
         def y_centre():
-            nc.vector.tensor_scalar(out=negc[:], in0=sy[:], scalar1=-1.0 / NS, scalar2=None, op0=ALU.mult)
-            nc.vector.tensor_tensor(out=ebias[:], in0=bias_sb[:, 32:36], in1=negc[:], op=ALU.add)
+            nc.vector.tensor_scalar(out=negc[:], in0=real["ytot"][:].rearrange("p (d w) -> p d w", w=2)[:, :, 0],
+                                    scalar1=-1.0 / NS, scalar2=None, op0=ALU.mult)
 
-        def y_spread(dt):
-            nc.scalar.activation(out=junk[:], in_=y_t[:, dt * 1024 : (dt + 1) * 1024], func=ACT.Square,
-                                 bias=negc[:, dt : dt + 1], accum_out=vsum[:, dt : dt + 1])
+        def y_diagonal(dt):
+            nc.vector.scalar_tensor_tensor(out=junk[:], in0=real["yprod"][:, dt * P : (dt + 1) * P], scalar=1.0 / NS,
+                                           in1=ident_f[:], op0=ALU.mult, op1=ALU.mult, accum_out=vsum[:, dt : dt + 1])
+
+        def y_bias():
+            nc.vector.tensor_tensor(out=ebias[:], in0=bias_sb[:, 32:36], in1=negc[:], op=ALU.add)
+            nc.vector.tensor_tensor(out=csq[:], in0=negc[:], in1=negc[:], op=ALU.mult)
 
         def y_variance():
-            nc.vector.tensor_scalar(out=vn[:], in0=vsum[:], scalar1=1.0 / NS, scalar2=None, op0=ALU.mult)
+            nc.vector.tensor_tensor(out=vn[:], in0=vsum[:], in1=csq[:], op=ALU.subtract)
 
-        for half in range(2):
-            op("ld:y%d" % half, "dma", DMA_CYCLES, 0, [], [YRAW], lambda half=half: load_rows("y_raw", y_samples, half))
         for dt in range(4):
-            bank = ("yps%d" % dt, "l2")
-            op("yt:%d" % dt, "pe", 500, RANK["y"] + dt * RANK["y_step"], ["ld:y0", "ld:y1"], [YRAW, bank],
-               lambda dt=dt: y_transposes(dt))
-            op("yc:%d" % dt, "act", 1060, RANK["y"] + dt * RANK["y_step"], ["yt:%d" % dt], [bank],
-               lambda dt=dt: y_copy(dt))
-            op("ys:%d" % dt, "act", 1060, RANK["ys"] + dt * RANK["y_step"], ["ycn"], [], lambda dt=dt: y_spread(dt))
-        op("ycn", "dve", 140, RANK["y"] + 4 * RANK["y_step"], ["bc"] + ["yc:%d" % dt for dt in range(4)], [], y_centre)
-        op("yv", "dve", 70, RANK["ys"] + 4 * RANK["y_step"], ["ys:%d" % dt for dt in range(4)], [], y_variance)
+            job("yt:%d" % dt, ["ld:y0", "ld:y1"], [("yps%d" % dt, "l2")], lambda dt=dt: y_transposes(dt))
+            job("yc:%d" % dt, ["yt:%d" % dt], [("yps%d" % dt, "l2")], lambda dt=dt: y_copy(dt))
+            job("yd:%d" % dt, ["yp"], [("yprod", "l2")], lambda dt=dt: y_diagonal(dt))
+        job("yp", ["ld:y0", "ld:y1"], [("yprod", "l2")], y_products)
+        job("ys", ["ld:y0", "ld:y1"], [("ytot", "red")], y_sums)
+        job("yn", ["ys"], [("ytot", "red")], y_centre)
+        job("yb", ["yn", "bc"], [], y_bias)
+        job("yv", ["yb"] + ["yd:%d" % dt for dt in range(4)], [], y_variance)
 
-        def w_name(layer, head, g):
-            return "%d%d%d" % (layer, head, g)
+        def w_regroup(c):
+            regroup(nc.scalar.copy if c in ON_SCALAR else nc.vector.tensor_copy, rot(wkey("grp", c), [P, 4 * c[3]], BF16, 64)[:], real[wkey("wraw", c)[0]][:])
 
-        def w_rank(layer, head, g):
-            if layer == 1:
-                return tau[(0, head, g)] - RANK["w1"]
-            return (RANK["w2mu"] if head == MU else RANK["w2lv"]) + g * RANK["w2_step"]
+        def w_quantise(c):
+            layer, head, s, w = c
+            sl = slice(s, s + w)
+            quantise(wc[(layer, head)][:, sl], ws[(layer, head)][:, sl], real[wkey("grp", c)[0]][:])
 
-        def w_load(layer, head, g):
-            raw = rot("raw" + w_name(layer, head, g), "wraw", [P, 2048], BF16)
-            r3 = raw[:].rearrange("p (t c) -> p t c", t=4)
-            if layer == 1:
-                src = w_dram[(1, head)].rearrange("(u q e) c -> u q e c", u=2, e=2)
-                for u in range(2):
-                    nc.sync.dma_start(out=r3[:, 2 * u : 2 * u + 2, :], in_=src[u, :, :, g * 512 : (g + 1) * 512])
-            else:
-                nc.sync.dma_start(
-                    out=r3, in_=w_dram[(2, head)][g * 512 : (g + 1) * 512, :].rearrange("(t p) d -> p t d", p=P)
-                )
+        for c in CHUNKS:
+            n = wname(c)
+            job("wr:" + n, ["ld:" + n], [wkey("wraw", c), wkey("grp", c)], lambda c=c: w_regroup(c))
+            job("wq:" + n, ["wr:" + n], [wkey("grp", c)], lambda c=c: w_quantise(c))
 
-        def w_regroup(layer, head, g, engine, tag):
-            n = w_name(layer, head, g)
-            regroup(engine, rot("grp" + n, tag, [P, 2048], BF16, 64)[:], real["raw" + n][:], 512)
-
-        def w_quantise(layer, head, g):
-            sl = slice(g * 512, (g + 1) * 512)
-            quantise(wc[(layer, head)][:, sl], ws[(layer, head)][:, sl], real["grp" + w_name(layer, head, g)][:])
-
-        chunks = sorted([(w_rank(layer, head, g), layer, head, g) for layer in (1, 2) for head in (MU, LV) for g in range(4)])
-        first_loads = ["ld:w" + w_name(*chunks[item][1:]) if isinstance(item, int) else "ld:" + item for item in FIRST_LOADS]
-        for rank, layer, head, g in chunks:
-            n = w_name(layer, head, g)
-            on_act = (layer, head, g) in SCALAR_REGROUP
-            raw = ("raw" + n, "wraw")
-            grp = ("grp" + n, "grps" if on_act else "grpv")
-            op("ld:w" + n, "dma", DMA_CYCLES, 0, [], [raw], lambda layer=layer, head=head, g=g: w_load(layer, head, g))
-            op("wr:" + n, "act" if on_act else "dve", 2058 if on_act else 1042, rank, ["ld:w" + n], [raw, grp],
-               lambda layer=layer, head=head, g=g, e=("act" if on_act else "dve"), tag=grp[1]: w_regroup(layer, head, g, e, tag))
-            op("wq:" + n, "dve", 526, rank, ["wr:" + n], [grp],
-               lambda layer=layer, head=head, g=g: w_quantise(layer, head, g))
-
-        def l1_pass(b, head, g, t):
-            w = BLOCKS[b]
-            acc = rot("a%d%d%d%d" % (b, head, g, t), "l1", [P, w], F32)
+        def l1_pass(unit, t):
+            head, g, b = unit
+            first, w = BLOCKS[b]
+            acc = rot(("a%d%d%d%d" % (head, g, b, t), "l1"), [P, w], F32)
             csl = slice(g * 512 + t * P, g * 512 + (t + 1) * P)
-            nsl = slice(OFFSETS[b], OFFSETS[b] + w)
+            nsl = slice(first, first + w)
             nc.tensor.matmul_mx(out=acc[:], lhsT=wc[(1, head)][:, csl].bitcast(FP8X4), lhsT_scale=ws[(1, head)][:, csl],
                                 rhs=xc[:, nsl].bitcast(FP8X4), rhs_scale=xs[:, nsl], start=True, stop=True)
 
-        def l1_exit(b, head, g, t):
-            w = BLOCKS[b]
-            hpl = rot("hpl%d%d%d" % (b, head, g), "hpl", [P, 4 * w], BF16)
+        def l1_exit(unit, t):
+            head, g, b = unit
+            w = BLOCKS[b][1]
+            hpl = rot(("hpl%d%d%d" % unit, "hpl"), [P, 4 * w], BF16)
             col = head * 16 + g * 4 + t
-            nc.scalar.activation(out=hpl[:, t * w : (t + 1) * w], in_=real["a%d%d%d%d" % (b, head, g, t)][:], func=ACT.Relu,
-                                 bias=bias_sb[:, col : col + 1])
+            nc.scalar.activation(out=hpl[:, t * w : (t + 1) * w], in_=real["a%d%d%d%d" % (head, g, b, t)][:],
+                                 func=ACT.Relu, bias=bias_sb[:, col : col + 1])
 
-        def h_regroup(b, head, g):
-            w = BLOCKS[b]
-            regroup("dve", rot("hg%d%d%d" % (b, head, g), "hg", [P, 4 * w], BF16, 64)[:], real["hpl%d%d%d" % (b, head, g)][:], w)
+        def h_regroup(unit):
+            w = BLOCKS[unit[2]][1]
+            regroup(nc.vector.tensor_copy, rot(("hg%d%d%d" % unit, "hg"), [P, 4 * w], BF16, 64)[:], real["hpl%d%d%d" % unit][:])
 
-        def h_quantise(b, head, g):
-            w = BLOCKS[b]
+        def h_quantise(unit):
+            head, g, b = unit
+            w = BLOCKS[b][1]
             sl = slice(g * w, (g + 1) * w)
-            quantise(hc[(head, b)][:, sl], hs[(head, b)][:, sl], real["hg%d%d%d" % (b, head, g)][:])
+            quantise(hc[(head, b)][:, sl], hs[(head, b)][:, sl], real["hg%d%d%d" % unit][:])
 
-        previous = None
-        for b, head, g in UNITS:
-            w = BLOCKS[b]
-            u = "%d%d%d" % (b, head, g)
-            hpl = ("hpl" + u, "hpl")
-            hg = ("hg" + u, "hg")
+        for unit in UNITS:
+            head, g, b = unit
+            u = "%d%d%d" % unit
             for t in range(4):
                 bank = ("a%s%d" % (u, t), "l1")
-                needs = ["wq:" + w_name(1, head, g), "xq:%d" % (1 if OFFSETS[b] >= 512 else 0)]
-                behind = [previous] if previous is not None else []
-                previous = "l1:%s:%d" % (u, t)
-                op(previous, "pe", max(w / 2.0 + 8, 74), tau[(b, head, g)] + 0.01 * t, needs, [bank],
-                   lambda b=b, head=head, g=g, t=t: l1_pass(b, head, g, t), behind)
-                op("ex:%s:%d" % (u, t), "act", w + 10, tau[(b, head, g)] + 0.01 * t, [previous, "bc"], [bank, hpl],
-                   lambda b=b, head=head, g=g, t=t: l1_exit(b, head, g, t))
-            op("hr:" + u, "dve", 2 * w + 18, tau[(b, head, g)] + RANK["h"], ["ex:%s:%d" % (u, t) for t in range(4)], [hpl, hg],
-               lambda b=b, head=head, g=g: h_regroup(b, head, g))
-            op("hq:" + u, "dve", w + 14, tau[(b, head, g)] + RANK["h"], ["hr:" + u], [hg],
-               lambda b=b, head=head, g=g: h_quantise(b, head, g))
+                needs = ["wq:1%d%d" % (head, g) + ("ab"[t // 2] if head == MU and g == 0 else ""), "xq:%d" % (BLOCKS[b][0] // 512)]
+                job("l1:%s:%d" % (u, t), needs, [bank], lambda unit=unit, t=t: l1_pass(unit, t))
+                job("ex:%s:%d" % (u, t), ["l1:%s:%d" % (u, t), "bc"], [bank, ("hpl" + u, "hpl")], lambda unit=unit, t=t: l1_exit(unit, t))
+            job("hr:" + u, ["ex:%s:%d" % (u, t) for t in range(4)], [("hpl" + u, "hpl"), ("hg" + u, "hg")], lambda unit=unit: h_regroup(unit))
+            job("hq:" + u, ["hr:" + u], [("hg" + u, "hg")], lambda unit=unit: h_quantise(unit))
+
+        def o_key(head, b, dt):
+            return ("o%d%d%d" % (head, b, dt), "l1" if (head, b) in LATE else "l2")
+
+        def red_key(b):
+            return ("red%d" % b, "red")
 
         def l2_pass(head, b, dt, g):
-            w = BLOCKS[b]
-            acc = rot("o%d%d%d" % (head, b, dt), "l2", [P, w], F32)
+            w = BLOCKS[b][1]
+            acc = rot(o_key(head, b, dt), [P, w], F32)
             wsl = slice(g * 512 + dt * P, g * 512 + (dt + 1) * P)
             hsl = slice(g * w, (g + 1) * w)
             nc.tensor.matmul_mx(out=acc[:], lhsT=wc[(2, head)][:, wsl].bitcast(FP8X4), lhsT_scale=ws[(2, head)][:, wsl],
                                 rhs=hc[(head, b)][:, hsl].bitcast(FP8X4), rhs_scale=hs[(head, b)][:, hsl],
                                 start=(g == 0), stop=(g == 3))
 
-        def kept(kind, b, dt):
-            w = BLOCKS[b]
-            if b == 0:
-                return rot("kept%s0" % kind, "big", [P, 2048], F32, 64)[:, dt * w : (dt + 1) * w]
-            base = 0 if kind == "e" else 4 * w
-            return rot("kept%d" % b, "big", [P, 2048], F32, 64)[:, base + dt * w : base + (dt + 1) * w]
-
-        def kept_key(kind, b):
-            return ("kept%s0" % kind if b == 0 else "kept%d" % b, "big")
+        def cols(b, dt):
+            first, w = BLOCKS[b]
+            return slice(dt * 1024 + first, dt * 1024 + first + w)
 
         def mu_delta(b, dt):
-            w = BLOCKS[b]
             nc.vector.scalar_tensor_tensor(
-                out=rot("dlt%d%d" % (b, dt), "dlt", [P, w], F32)[:], in0=real["o%d%d%d" % (MU, b, dt)][:],
-                scalar=bias_sb[:, 32 + dt : 33 + dt], in1=y_t[:, dt * 1024 + OFFSETS[b] : dt * 1024 + OFFSETS[b] + w],
-                op0=ALU.add, op1=ALU.subtract)
+                out=rot(("dlt%d%d" % (b, dt), "dlt"), [P, 512], F32)[:], in0=real["o%d%d%d" % (MU, b, dt)][:],
+                scalar=bias_sb[:, 32 + dt : 33 + dt], in1=y_t[:, cols(b, dt)], op0=ALU.add, op1=ALU.subtract)
 
         def mu_centred_square(b, dt):
-            nc.scalar.activation(out=kept("e", b, dt), in_=real["o%d%d%d" % (MU, b, dt)][:], func=ACT.Square,
+            nc.scalar.activation(out=sq_e()[:, cols(b, dt)], in_=real["o%d%d%d" % (MU, b, dt)][:], func=ACT.Square,
                                  bias=ebias[:, dt : dt + 1])
 
         def mu_delta_square(b, dt):
-            nc.scalar.activation(out=kept("s", b, dt), in_=real["dlt%d%d" % (b, dt)][:], func=ACT.Square)
+            nc.scalar.activation(out=sq_d[:, cols(b, dt)], in_=real["dlt%d%d" % (b, dt)][:], func=ACT.Square)
 
         def lv_tanh(b, dt):
-            nc.scalar.activation(out=rot("th%d%d" % (b, dt), "th", [P, BLOCKS[b]], F32)[:], in_=real["o%d%d%d" % (LV, b, dt)][:],
-                                 func=ACT.Tanh, bias=bias_sb[:, 36 + dt : 37 + dt])
+            nc.scalar.activation(out=rot(("th%d%d" % (b, dt), "th"), [P, BLOCKS[b][1]], F32)[:],
+                                 in_=real["o%d%d%d" % (LV, b, dt)][:], func=ACT.Tanh, bias=bias_sb[:, 36 + dt : 37 + dt])
 
         def lv_exp(b, dt):
-            nc.scalar.activation(out=rot("wgt%d%d" % (b, dt), "wgt", [P, BLOCKS[b]], F32)[:], in_=real["th%d%d" % (b, dt)][:],
-                                 func=ACT.Exp, scale=-1.0)
+            nc.scalar.activation(out=rot(("wgt%d%d" % (b, dt), "wgt"), [P, BLOCKS[b][1]], F32)[:],
+                                 in_=real["th%d%d" % (b, dt)][:], func=ACT.Exp, scale=-1.0)
 
         def product(which, b, dt):
-            out = rot("p%d%d%d" % (which, b, dt), "p%d" % which, [P, BLOCKS[b]], F32)
+            out = rot(("p%d%d%d" % (which, b, dt), "p%d" % which), [P, BLOCKS[b][1]], F32)
             if which == 1:
-                nc.vector.tensor_tensor(out=out[:], in0=kept("s", b, dt), in1=real["wgt%d%d" % (b, dt)][:], op=ALU.mult)
+                nc.vector.tensor_tensor(out=out[:], in0=sq_d[:, cols(b, dt)], in1=real["wgt%d%d" % (b, dt)][:], op=ALU.mult)
             else:
-                nc.vector.scalar_tensor_tensor(out=out[:], in0=kept("e", b, dt), scalar=vn[:, dt : dt + 1],
+                nc.vector.scalar_tensor_tensor(out=out[:], in0=sq_e()[:, cols(b, dt)], scalar=vn[:, dt : dt + 1],
                                                in1=real["wgt%d%d" % (b, dt)][:], op0=ALU.add, op1=ALU.mult)
 
         def pair_sum(which, b, dt):
-            nc.vector.tensor_tensor(out=rot("s%d%d%d" % (which, b, dt), "s%d" % which, [P, BLOCKS[b]], F32)[:],
-                                    in0=real["p%d%d%d" % (which, b, dt - 1)][:], in1=real["p%d%d%d" % (which, b, dt)][:], op=ALU.add)
+            here = real["p%d%d%d" % (which, b, dt)][:]
+            nc.vector.tensor_tensor(out=here, in0=real["p%d%d%d" % (which, b, dt - 1)][:], in1=here, op=ALU.add)
 
-        def reduce_d(which, b, dt, src, first, last):
-            nc.tensor.matmul(out=rot("red%d" % b, "red", [P, BLOCKS[b]], F32)[:], lhsT=sel[which - 1][:], rhs=real[src][:],
-                             start=first, stop=last)
+        def reduce_d(which, b, dt, first, last):
+            nc.tensor.matmul(out=rot(red_key(b), [P, BLOCKS[b][1]], F32)[:], lhsT=sel[which - 1][:],
+                             rhs=real["p%d%d%d" % (which, b, dt)][:], start=first, stop=last)
 
         def result(b):
-            nc.scalar.copy(out=rot("res%d" % b, "res", [P, BLOCKS[b]], F32)[:], in_=real["red%d" % b][:])
+            nc.scalar.copy(out=res[b][:], in_=real["red%d" % b][:])
 
         def store(b):
+            first, w = BLOCKS[b]
             for which in range(2):
-                nc.sync.dma_start(out=outs[which][OFFSETS[b] : OFFSETS[b] + BLOCKS[b]].rearrange("(o n) -> o n", o=1),
-                                  in_=real["res%d" % b][which : which + 1, :])
+                nc.sync.dma_start(out=outs[which][first : first + w].rearrange("(o n) -> o n", o=1), in_=res[b][which : which + 1, :])
 
-        for b in range(len(BLOCKS)):
-            w = BLOCKS[b]
-            step = RANK["d_step"] * w / 512.0
-            red = ("red%d" % b, "red")
-            reduces = []
-            for dt in range(4):
-                for head in (MU, LV):
-                    bank = ("o%d%d%d" % (head, b, dt), "l2")
+        for head in (MU, LV):
+            for b in OF_HEAD[head]:
+                for dt in range(4):
+                    n = "%d%d" % (b, dt)
                     for g in range(4):
-                        needs = ["wq:" + w_name(2, head, g), "hq:%d%d%d" % (b, head, g)]
-                        behind = ["l2:%d%d%d:%d" % (head, b, dt, g - 1)] if g > 0 else []
-                        if g == 0 and (head, b) not in OPEN_EARLY:
-                            needs.extend(["wq:" + w_name(2, head, 3), "hq:%d%d%d" % (b, head, 3)])
-                        op("l2:%d%d%d:%d" % (head, b, dt, g), "pe", max(w / 2.0 + 8, 74), after(head, b) + RANK["l2_%d%d" % (head, b)] + dt * step,
-                           needs, [bank], lambda head=head, b=b, dt=dt, g=g: l2_pass(head, b, dt, g), behind)
+                        job("l2:%d%s:%d" % (head, n, g), ["wq:2%d%d" % (head, g), "hq:%d%d%d" % (head, g, b)] + ["l2:%d%s:%d" % (head, n, g - 1)] * (g > 0), [o_key(head, b, dt)],
+                            lambda head=head, b=b, dt=dt, g=g: l2_pass(head, b, dt, g))
+        for b in OF_HEAD[MU]:
+            for dt in range(4):
                 n = "%d%d" % (b, dt)
-                mbank = ("o%d%d%d" % (MU, b, dt), "l2")
-                lbank = ("o%d%d%d" % (LV, b, dt), "l2")
-                rank = after(MU, b) + RANK["mu%d" % b] + dt * step
-                op("md:" + n, "dve", w + 15, rank, ["l2:%d%d%d:3" % (MU, b, dt), "yc:%d" % dt], [mbank, ("dlt" + n, "dlt")],
-                   lambda b=b, dt=dt: mu_delta(b, dt))
-                op("me:" + n, "act", w + 10, rank, ["l2:%d%d%d:3" % (MU, b, dt), "ycn"], [mbank, kept_key("e", b)],
-                   lambda b=b, dt=dt: mu_centred_square(b, dt))
-                op("ms:" + n, "act", w + 10, rank, ["md:" + n], [("dlt" + n, "dlt"), kept_key("s", b)],
-                   lambda b=b, dt=dt: mu_delta_square(b, dt))
-                rank = after(LV, b) + RANK["lv%d" % b] + dt * step
-                op("lt:" + n, "act", w + 10, rank, ["l2:%d%d%d:3" % (LV, b, dt)], [lbank, ("th" + n, "th")],
-                   lambda b=b, dt=dt: lv_tanh(b, dt))
-                op("lx:" + n, "act", w + 10, rank, ["lt:" + n], [("th" + n, "th"), ("wgt" + n, "wgt")],
-                   lambda b=b, dt=dt: lv_exp(b, dt))
+                mk = o_key(MU, b, dt)
+                job("md:" + n, ["l2:0%s:3" % n, "yc:%d" % dt], [mk, ("dlt" + n, "dlt")], lambda b=b, dt=dt: mu_delta(b, dt))
+                job("me:" + n, ["l2:0%s:3" % n, "yb"], [mk, ("sq_e", "xbig")], lambda b=b, dt=dt: mu_centred_square(b, dt))
+                job("ms:" + n, ["md:" + n], [("dlt" + n, "dlt")], lambda b=b, dt=dt: mu_delta_square(b, dt))
+        reduces = {}
+        for b in OF_HEAD[LV]:
+            reduces[b] = [(which, dt) for dt in range(4) for which in (1, 2) if (b, dt + 1) not in PAIRED]
+            for dt in range(4):
+                n = "%d%d" % (b, dt)
+                m = "%d%d" % (BLOCKS[b][0] // 512, dt)
+                wk = ("wgt" + n, "wgt")
+                job("lt:" + n, ["l2:1%s:3" % n], [o_key(LV, b, dt), ("th" + n, "th")], lambda b=b, dt=dt: lv_tanh(b, dt))
+                job("lx:" + n, ["lt:" + n], [("th" + n, "th"), wk], lambda b=b, dt=dt: lv_exp(b, dt))
+                job("p1:" + n, ["lx:" + n, "ms:" + m], [wk, ("p1" + n, "p1")], lambda b=b, dt=dt: product(1, b, dt))
+                job("p2:" + n, ["lx:" + n, "me:" + m, "yv"], [wk, ("p2" + n, "p2"), ("sq_e", "xbig")], lambda b=b, dt=dt: product(2, b, dt))
                 for which in (1, 2):
-                    rank = after(LV, b) + RANK["p%d" % b] + dt * step
-                    pk = ("p%d%s" % (which, n), "p%d" % which)
-                    needs = ["lx:" + n, "ms:" + n] if which == 1 else ["lx:" + n, "me:" + n, "yv"]
-                    op("p%d:%s" % (which, n), "dve", w + 15, rank, needs,
-                       [pk, ("wgt" + n, "wgt"), kept_key("s" if which == 1 else "e", b)],
-                       lambda which=which, b=b, dt=dt: product(which, b, dt))
-                    rrank = after(LV, b) + RANK["r%d" % b] + dt * step
-                    first = which == 1 and dt == (1 if PAIR_ADD[b] else 0)
-                    last = which == 2 and dt == 3
-                    if not PAIR_ADD[b]:
-                        op("r%d:%s" % (which, n), "pe", 2 * w, rrank, ["p%d:%s" % (which, n)], [pk, red],
-                           lambda which=which, b=b, dt=dt, first=first, last=last: reduce_d(
-                               which, b, dt, "p%d%d%d" % (which, b, dt), first, last), reduces[-1:])
-                        reduces.append("r%d:%s" % (which, n))
-                    elif dt % 2 == 1:
-                        sk = ("s%d%s" % (which, n), "s%d" % which)
-                        op("a%d:%s" % (which, n), "dve", w + 15, rank, ["p%d:%s" % (which, n), "p%d:%d%d" % (which, b, dt - 1)],
-                           [pk, ("p%d%d%d" % (which, b, dt - 1), "p%d" % which), sk],
-                           lambda which=which, b=b, dt=dt: pair_sum(which, b, dt))
-                        op("r%d:%s" % (which, n), "pe", 2 * w, rrank, ["a%d:%s" % (which, n)], [sk, red],
-                           lambda which=which, b=b, dt=dt, first=first, last=last: reduce_d(
-                               which, b, dt, "s%d%d%d" % (which, b, dt), first, last), reduces[-1:])
-                        reduces.append("r%d:%s" % (which, n))
-            rank = after(LV, b) + RANK["r%d" % b] + 4 * step
-            op("res:%d" % b, "act", w + 10, rank, reduces[-1:], [red, ("res%d" % b, "res")], lambda b=b: result(b))
-            op("st:%d" % b, "dma", 20, rank, ["res:%d" % b], [("res%d" % b, "res")], lambda b=b: store(b))
+                    last = ["p%d:%s" % (which, n)]
+                    if (b, dt) in PAIRED:
+                        before = "%d%d" % (b, dt - 1)
+                        job("a%d:%s" % (which, n), ["p%d:%s" % (which, before)] + last,
+                            [("p%d%s" % (which, before), "p%d" % which), ("p%d%s" % (which, n), "p%d" % which)],
+                            lambda which=which, b=b, dt=dt: pair_sum(which, b, dt))
+                        last = ["a%d:%s" % (which, n)]
+                    if (which, dt) in reduces[b]:
+                        at = reduces[b].index((which, dt))
+                        last = last + ["r%d:%d%d" % (reduces[b][at - 1][0], b, reduces[b][at - 1][1])] * (at > 0)
+                        job("r%d:%s" % (which, n), last, [("p%d%s" % (which, n), "p%d" % which), red_key(b)],
+                            lambda which=which, b=b, dt=dt, at=at: reduce_d(which, b, dt, at == 0, at == len(reduces[b]) - 1))
+            job("rs:%d" % b, ["r%d:%d%d" % (which, b, dt) for which, dt in reduces[b]], [red_key(b)], lambda b=b: result(b))
+            job("st:%d" % b, ["rs:%d" % b], [], lambda b=b: store(b))
 
-        loads = [r for r in records if r["engine"] == "dma"]
-        rest = [r for r in records if r["engine"] != "dma"]
-        head_loads = [r for n in first_loads for r in loads if r["name"] == n]
-        tail_loads = [r for r in loads if r["name"] not in first_loads]
-        order = plan(head_loads + tail_loads + rest, SLOTS)
+        rank = {}
+        clock = 0.0
+        tau = {}
+        for unit in UNITS:
+            tau[unit] = clock
+            clock = clock + BLOCKS[unit[2]][1] / 512.0
+        end_of = {}
+        for unit in UNITS:
+            end_of[(unit[0], unit[2])] = tau[unit] + BLOCKS[unit[2]][1] / 512.0
+
+        def put(n, r):
+            rank[n] = r
+
+        put("bt", -4)
+        put("bc", -4)
+        for half in range(2):
+            for pair in range(2):
+                put("xt:%d%d" % (half, pair), X_RANK[half])
+                put("xc:%d%d" % (half, pair), X_RANK[half])
+            put("xq:%d" % half, X_RANK[half])
+        for dt in range(4):
+            put("yt:%d" % dt, Y_RANK + 0.1 * dt)
+            put("yc:%d" % dt, Y_RANK + 0.1 * dt)
+            put("yd:%d" % dt, Y_RANK + 2 + 0.1 * dt)
+        put("ys", Y_RANK + 0.5)
+        put("yp", Y_RANK + 0.5)
+        put("yn", Y_RANK + 1)
+        put("yb", Y_RANK + 1)
+        put("yv", Y_RANK + 3)
+        for c in CHUNKS:
+            layer, head, s, w = c
+            if layer == 1:
+                r = min(tau[unit] for unit in UNITS if unit[0] == head and unit[1] == s // 512) - W1_AHEAD
+            else:
+                r = W2_RANK[head] + W2_STEP[head] * (s // 512)
+            put("wr:" + wname(c), r - (RA_AHEAD if c in ON_SCALAR else 0))
+            put("wq:" + wname(c), r)
+        for unit in UNITS:
+            head, g, b = unit
+            u = "%d%d%d" % unit
+            for t in range(4):
+                put("l1:%s:%d" % (u, t), tau[unit] + 0.01 * t)
+                put("ex:%s:%d" % (u, t), tau[unit] + 0.01 * t)
+            put("hr:" + u, tau[unit] + H_BEHIND)
+            put("hq:" + u, tau[unit] + H_BEHIND)
+        for head in (MU, LV):
+            for b in OF_HEAD[head]:
+                step = STEP * BLOCKS[b][1] / 512.0
+                due = end_of[(head, b)] + BEHIND[(head, b)]
+                for dt in range(4):
+                    n = "%d%d" % (b, dt)
+                    for g in range(4):
+                        put("l2:%d%s:%d" % (head, n, g), due + step * dt - 1)
+                    for job_name in ("md:", "me:", "ms:") if head == MU else ("lt:", "lx:", "p1:", "p2:", "a1:", "a2:", "r1:", "r2:"):
+                        put(job_name + n, due + step * dt)
+                if head == LV:
+                    put("rs:%d" % b, due + 4 * step)
+                    put("st:%d" % b, due + 4 * step)
+        for i, n in enumerate(LOADS):
+            put("ld:" + n, -19 + 0.01 * i)
+
+        users = {}
+        for n in jobs:
+            for key in jobs[n][1]:
+                users[key] = users.get(key, 0) + 1
+        left = sorted(jobs, key=lambda n: rank[n])
+        done = set()
+        live = {}
+
+        def write(n):
+            needs, tiles, emit = jobs[n]
+            for key in tiles:
+                if key not in live.get(key[1], []):
+                    live[key[1]] = live.get(key[1], []) + [key]
+            emit()
+            done.add(n)
+            left.remove(n)
+            for key in tiles:
+                users[key] = users[key] - 1
+                if users[key] == 0:
+                    live[key[1]].remove(key)
 
         with tc.manual_schedule():
-            for start, name in order:
-                emitters[name]()
+            for n in HEAD:
+                write(n)
+        while left:
+            for n in left:
+                needs, tiles, emit = jobs[n]
+                if not all(m in done for m in needs):
+                    continue
+                fresh = [key for key in tiles if key not in live.get(key[1], [])]
+                if all(len(live.get(key[1], [])) < SLOTS[key[1]] for key in fresh):
+                    break
+            else:
+                assert False, left[:5]
+            write(n)

@@ -18,7 +18,7 @@ NS = 1024
 MU = 0
 LV = 1
 
-SLOTS = {"xbig": 1, "wraw": 5, "wraws": 2, "grp": 3, "hpl": 4, "hg": 3, "l1": 4, "l2": 3, "red": 1,
+SLOTS = {"xbig": 1, "wraw": 5, "wraws": 2, "grp": 2, "grps": 1, "hpl": 5, "hg": 2, "l1": 4, "l2": 3, "red": 1,
          "dlt": 3, "th": 2, "wgt": 4, "p1": 3, "p2": 3}
 
 BLOCKS = ((0, 512), (512, 512), (512, 256), (768, 256))
@@ -29,19 +29,11 @@ CHUNKS = [(1, MU, 0, 256), (1, MU, 256, 256)] + [(1, MU, s, 512) for s in (512, 
     (layer, head, s, 512) for layer, head in ((1, LV), (2, MU), (2, LV)) for s in (0, 512, 1024, 1536)
 ]
 ON_SCALAR = ((2, MU, 0, 512), (2, MU, 512, 512), (2, MU, 1024, 512))
-PAIRED = ((0, 3), (2, 1), (2, 3), (3, 1), (3, 3))
-LATE = ()
-HEAD = ("ld:x00", "ld:x01", "ld:100a", "ld:bias", "ld:100b", "xt:00", "xt:01", "xc:00", "xc:01", "bt", "wr:100a", "wq:100a", "bc", "xq:0", "wr:100b", "wq:100b", "l1:000:0", "l1:000:1", "l1:000:2", "l1:000:3")
-LOADS = ("x00", "x01", "100a", "bias", "100b", "101", "102", "103", "110", "111", "112", "113", "200", "x1", "201", "y0", "y1", "202", "203", "210", "211", "212", "213")
-X_RANK = (-10, 2)
-Y_RANK = 4
-W1_AHEAD = 3
-W2_RANK = {MU: 6, LV: 8}
-W2_STEP = {MU: 1, LV: 1}
-RA_AHEAD = 0
-H_BEHIND = 5
+PAIRED = ((0, 1), (0, 3), (2, 1), (2, 3), (3, 1), (3, 3))
+LATE = ((LV, 2), (LV, 3))
+LOADS = ("x00", "x01", "100a", "100b", "101", "102", "103", "110", "200", "x1", "111", "112", "y0", "y1", "201", "113", "203", "202", "210", "211", "212", "213")
 STEP = 1
-BEHIND = {(MU, 0): 6, (MU, 1): 3, (LV, 0): 4, (LV, 2): 3, (LV, 3): 3}
+BEHIND = {(MU, 0): 6, (MU, 1): 3, (LV, 0): 4, (LV, 2): 2, (LV, 3): 4}
 
 
 def tile_infoncemi_pa_kernel(
@@ -59,27 +51,35 @@ def tile_infoncemi_pa_kernel(
         const = ctx.enter_context(tc.tile_pool(name="const", bufs=1))
         keep = ctx.enter_context(tc.tile_pool(name="keep", bufs=1))
         pools = {}
-        for tag in ("xbig", "wraw", "wraws", "grp", "hpl", "hg", "dlt", "th", "wgt", "p1", "p2"):
-            pools[tag] = ctx.enter_context(tc.tile_pool(name="pool_" + tag, bufs=SLOTS[tag]))
+        for tag in ("xbig", "wraw", "wraws", "grp", "grps", "hpl", "hg", "dlt", "th", "wgt", "p1", "p2"):
+            pools[tag] = ctx.enter_context(tc.tile_pool(name="pool_" + tag, bufs=1))
         for tag in ("l1", "l2", "red"):
-            pools[tag] = ctx.enter_context(tc.psum_pool(name="psum_" + tag, bufs=SLOTS[tag]))
+            pools[tag] = ctx.enter_context(tc.psum_pool(name="psum_" + tag, bufs=1))
         real = {}
+        turn = {}
 
         def rot(key, shape, dtype, align=None):
             name, tag = key
             if name not in real:
+                turn[tag] = turn.get(tag, -1) + 1
+                slot = "%s_%d" % (tag, turn[tag] % SLOTS[tag])
                 if align is None:
-                    real[name] = pools[tag].tile(shape, dtype, tag=tag, name=name)
+                    real[name] = pools[tag].tile(shape, dtype, tag=slot, name=name)
                 else:
-                    real[name] = pools[tag].tile(shape, dtype, tag=tag, name=name, align_bytes=align)
+                    real[name] = pools[tag].tile(shape, dtype, tag=slot, name=name, align_bytes=align)
             return real[name]
 
+        ctx.enter_context(tc.manual_schedule())
+        btile = const.tile([P, P], BF16)
+        nc.vector.memset(btile[:], 0.0)
+        nc.scalar.dma_start(out=btile[0:16, :], in_=mu_b1.rearrange("(r p) -> r p", p=P))
+        nc.scalar.dma_start(out=btile[16:32, :], in_=lv_b1.rearrange("(r p) -> r p", p=P))
+        nc.scalar.dma_start(out=btile[32:36, :], in_=mu_b2.rearrange("(r p) -> r p", p=P))
+        nc.scalar.dma_start(out=btile[36:40, :], in_=lv_b2.rearrange("(r p) -> r p", p=P))
         warm = const.tile([P, 1], F32)
         nc.vector.memset(warm[:], 0.0)
         warm2 = const.tile([P, 1], F32)
         nc.scalar.activation(out=warm2[:], in_=warm[:], func=ACT.Tanh)
-        btile = const.tile([P, P], BF16)
-        nc.vector.memset(btile[:], 0.0)
         ident_f = const.tile([P, P], F32)
         make_identity(nc, ident_f[:])
         ident_bf = const.tile([P, P], BF16)
@@ -127,12 +127,6 @@ def tile_infoncemi_pa_kernel(
         def quantise(codes, plane, grouped):
             nc.vector.quantize_mx(out=codes.bitcast(FP8X4), scales=plane, in_=grouped)
 
-        def bias_load():
-            nc.sync.dma_start(out=btile[0:16, :], in_=mu_b1.rearrange("(r p) -> r p", p=P))
-            nc.sync.dma_start(out=btile[16:32, :], in_=lv_b1.rearrange("(r p) -> r p", p=P))
-            nc.sync.dma_start(out=btile[32:36, :], in_=mu_b2.rearrange("(r p) -> r p", p=P))
-            nc.sync.dma_start(out=btile[36:40, :], in_=lv_b2.rearrange("(r p) -> r p", p=P))
-
         def load_rows(tile, src, r0, rows):
             nc.sync.dma_start(
                 out=tile[:, r0 * 512 : (r0 + rows) * 512].rearrange("p (r k) -> p r k", r=rows),
@@ -149,7 +143,7 @@ def tile_infoncemi_pa_kernel(
             return "%d%d%d" % (c[0], c[1], c[2] // 512) + ("" if c[3] == 512 else "ab"[c[2] // 256])
 
         def wkey(kind, c):
-            return (kind + wname(c), "wraws" if kind == "wraw" and c in ON_SCALAR else kind)
+            return (kind + wname(c), kind + "s" if c in ON_SCALAR else kind)
 
         def w_load(c):
             layer, head, s, w = c
@@ -164,7 +158,6 @@ def tile_infoncemi_pa_kernel(
                     out=r3, in_=w_dram[(2, head)][s : s + w, :].rearrange("(t p) d -> p t d", p=P)
                 )
 
-        job("ld:bias", [], [], bias_load)
         for half in range(2):
             job("ld:y%d" % half, [], [], lambda half=half: load_rows(y_raw, y_samples, 4 * half, 4))
         for n, r0, rows in (("x00", 0, 2), ("x01", 2, 2), ("x1", 4, 4)):
@@ -178,7 +171,7 @@ def tile_infoncemi_pa_kernel(
         def bias_copy():
             nc.vector.tensor_copy(out=bias_sb[:], in_=real["bias_t"][:, 0:40])
 
-        job("bt", ["ld:bias"], [("bias_t", "red")], bias_transpose)
+        job("bt", [], [("bias_t", "red")], bias_transpose)
         job("bc", ["bt"], [("bias_t", "red")], bias_copy)
 
         def x_transposes(half, pair):
@@ -314,10 +307,10 @@ def tile_infoncemi_pa_kernel(
             job("hq:" + u, ["hr:" + u], [("hg" + u, "hg")], lambda unit=unit: h_quantise(unit))
 
         def o_key(head, b, dt):
-            return ("o%d%d%d" % (head, b, dt), "l1" if (head, b) in LATE else "l2")
+            return ("o%d%d%d" % (head, b, dt), "l1" if (head, b) in LATE and (b, dt) >= (2, 2) else "l2")
 
         def red_key(b):
-            return ("red%d" % b, "red")
+            return ("red%d" % b, "l2" if b == 3 else "red")
 
         def l2_pass(head, b, dt, g):
             w = BLOCKS[b][1]
@@ -417,99 +410,92 @@ def tile_infoncemi_pa_kernel(
             job("rs:%d" % b, ["r%d:%d%d" % (which, b, dt) for which, dt in reduces[b]], [red_key(b)], lambda b=b: result(b))
             job("st:%d" % b, ["rs:%d" % b], [], lambda b=b: store(b))
 
-        rank = {}
-        clock = 0.0
-        tau = {}
-        for unit in UNITS:
-            tau[unit] = clock
-            clock = clock + BLOCKS[unit[2]][1] / 512.0
-        end_of = {}
-        for unit in UNITS:
-            end_of[(unit[0], unit[2])] = tau[unit] + BLOCKS[unit[2]][1] / 512.0
+        name = ["%d%d%d" % unit for unit in UNITS]
 
-        def put(n, r):
-            rank[n] = r
+        def l1(u):
+            return ["l1:%s:%d" % (name[u], t) for t in range(4)]
 
-        put("bt", -4)
-        put("bc", -4)
-        for half in range(2):
-            for pair in range(2):
-                put("xt:%d%d" % (half, pair), X_RANK[half])
-                put("xc:%d%d" % (half, pair), X_RANK[half])
-            put("xq:%d" % half, X_RANK[half])
-        for dt in range(4):
-            put("yt:%d" % dt, Y_RANK + 0.1 * dt)
-            put("yc:%d" % dt, Y_RANK + 0.1 * dt)
-            put("yd:%d" % dt, Y_RANK + 2 + 0.1 * dt)
-        put("ys", Y_RANK + 0.5)
-        put("yp", Y_RANK + 0.5)
-        put("yn", Y_RANK + 1)
-        put("yb", Y_RANK + 1)
-        put("yv", Y_RANK + 3)
-        for c in CHUNKS:
-            layer, head, s, w = c
-            if layer == 1:
-                r = min(tau[unit] for unit in UNITS if unit[0] == head and unit[1] == s // 512) - W1_AHEAD
-            else:
-                r = W2_RANK[head] + W2_STEP[head] * (s // 512)
-            put("wr:" + wname(c), r - (RA_AHEAD if c in ON_SCALAR else 0))
-            put("wq:" + wname(c), r)
-        for unit in UNITS:
-            head, g, b = unit
-            u = "%d%d%d" % unit
-            for t in range(4):
-                put("l1:%s:%d" % (u, t), tau[unit] + 0.01 * t)
-                put("ex:%s:%d" % (u, t), tau[unit] + 0.01 * t)
-            put("hr:" + u, tau[unit] + H_BEHIND)
-            put("hq:" + u, tau[unit] + H_BEHIND)
-        for head in (MU, LV):
-            for b in OF_HEAD[head]:
-                step = STEP * BLOCKS[b][1] / 512.0
-                due = end_of[(head, b)] + BEHIND[(head, b)]
-                for dt in range(4):
-                    n = "%d%d" % (b, dt)
-                    for g in range(4):
-                        put("l2:%d%s:%d" % (head, n, g), due + step * dt - 1)
-                    for job_name in ("md:", "me:", "ms:") if head == MU else ("lt:", "lx:", "p1:", "p2:", "a1:", "a2:", "r1:", "r2:"):
-                        put(job_name + n, due + step * dt)
-                if head == LV:
-                    put("rs:%d" % b, due + 4 * step)
-                    put("st:%d" % b, due + 4 * step)
-        for i, n in enumerate(LOADS):
-            put("ld:" + n, -19 + 0.01 * i)
+        def ex(u):
+            return ["ex:%s:%d" % (name[u], t) for t in range(4)]
 
+        def l2(n):
+            return ["l2:%s:%d" % (n, g) for g in range(4)]
+
+        def th(n):
+            return ["lt:" + n, "lx:" + n]
+
+        def pr(n):
+            return ["p1:" + n, "p2:" + n] + (["a1:" + n, "a2:" + n] if (int(n[0]), int(n[1])) in PAIRED else [])
+
+        def rd(n):
+            return ["r%d:%s" % (which, n) for which in (1, 2) if (which, int(n[1])) in reduces[int(n[0])]]
+
+        sync = ["ld:" + n for n in LOADS] + ["st:0", "st:2", "st:3"]
+
+        stream = ["110", 0, "111", 1, "112", 2, "113", 3, "203", 4, "210", 5, "211", 6, "212", 7, "213", 8, 9, 10, 11, 12, 13, 14, 15, 16, 17, 18, 19]
+        extra = {"111": ["wq:200"], "113": ["xq:1"], "203": ["wq:201", "yn"], 4: ["yb"], "210": ["yd:0"], 5: ["wq:202", "yd:1"], "211": ["yd:2"], 6: ["yd:3", "md:00"],
+                 "212": ["md:01"], 7: ["md:02"], "213": ["md:03", "yv"], 10: pr("00"), 11: ["p1:01", "p2:01"], 12: ["a1:01", "a2:01", "p1:02", "p2:02"], 13: [],
+                 14: ["md:10", "p1:03", "p2:03"], 15: ["md:11", "a1:03", "a2:03"], 16: ["md:12"], 17: ["md:13"], 18: pr("20"), 19: pr("21")}
+        vector = ["wr:100a", "wq:100a", "xq:0", "wr:100b", "bc", "wq:100b", "wr:101", "wq:101", "wr:102", "wq:102", "wr:103", "wq:103"]
+
+        def stage(kind, item):
+            return ("w" if item in LOADS else "h") + kind + ":" + (item if item in LOADS else name[item])
+
+        vector += [stage("r", stream[0])]
+        for item, following in zip(stream, stream[1:] + [None]):
+            ahead = [stage("r", following)] if following is not None else []
+            vector += ahead + [stage("q", item)] + extra.get(item, [])
+
+        scalar_behind = {2: ["wr:200"], 3: ["xc:10", "xc:11", "wr:201"], 4: ["yc:0", "yc:1"], 5: ["yc:2", "yc:3"], 6: ["wr:202"],
+                         8: ["me:00", "me:01"], 9: ["ms:00", "me:02", "ms:01"], 10: ["me:03", "ms:02"],
+                         11: ["ms:03"] + th("00"), 12: th("01"), 13: ["lt:02"], 14: ["lx:02", "lt:03"],
+                         15: ["lx:03", "me:10"], 16: ["me:11", "ms:10"], 17: ["me:12", "ms:11"], 18: ["me:13", "ms:12"], 19: ["lt:20", "lt:21", "lx:20", "lx:21", "ms:13", "rs:0"]}
+        tensor_behind = {3: ["xt:10", "xt:11"], 4: ["yt:0", "yt:1", "yt:2", "ys"], 5: ["yt:3", "yp"],
+                         8: l2("000") + l2("001"), 9: l2("002"), 10: l2("003"), 11: l2("100"), 12: l2("101"), 13: l2("102"), 14: l2("103"),
+                         15: l2("010") + rd("01"), 16: l2("011"), 17: l2("012"), 18: l2("013") + l2("120"), 19: l2("121") + rd("03")}
+        tensor = ["xt:00", "xt:01", "bt"]
+        scalar = ["xc:00", "xc:01"]
+        for u in range(len(UNITS)):
+            tensor += l1(u) + tensor_behind.get(u, [])
+            scalar += ex(u) + scalar_behind.get(u, [])
+        rest = ["22", "23", "30", "31", "32", "33"]
+        scalar += ["lt:" + rest[0]]
+        for n, following in zip(rest, rest[1:] + [None]):
+            scalar += (["lt:" + following] if following is not None else []) + ["lx:" + n]
+        for n in rest:
+            vector += pr(n)
+        tensor += l2("122") + l2("123") + l2("130") + l2("131") + l2("132") + l2("133") + rd("21") + rd("23")
+        tensor += rd("31") + rd("33")
+        scalar += ["rs:2", "rs:3"]
+
+        queues = [sync, tensor, scalar, vector]
         users = {}
-        for n in jobs:
-            for key in jobs[n][1]:
-                users[key] = users.get(key, 0) + 1
-        left = sorted(jobs, key=lambda n: rank[n])
+        for queue in queues:
+            for n in queue:
+                for key in jobs[n][1]:
+                    users[key] = users.get(key, 0) + 1
         done = set()
-        live = {}
-
-        def write(n):
-            needs, tiles, emit = jobs[n]
-            for key in tiles:
-                if key not in live.get(key[1], []):
-                    live[key[1]] = live.get(key[1], []) + [key]
-            emit()
-            done.add(n)
-            left.remove(n)
-            for key in tiles:
-                users[key] = users[key] - 1
-                if users[key] == 0:
-                    live[key[1]].remove(key)
-
-        with tc.manual_schedule():
-            for n in HEAD:
-                write(n)
-        while left:
-            for n in left:
+        taken = {}
+        at = [0, 0, 0, 0]
+        moved = True
+        while moved:
+            moved = False
+            for q, queue in enumerate(queues):
+                if at[q] >= len(queue):
+                    continue
+                n = queue[at[q]]
                 needs, tiles, emit = jobs[n]
                 if not all(m in done for m in needs):
                     continue
-                fresh = [key for key in tiles if key not in live.get(key[1], [])]
-                if all(len(live.get(key[1], [])) < SLOTS[key[1]] for key in fresh):
-                    break
-            else:
-                assert False, left[:5]
-            write(n)
+                fresh = [key for key in tiles if key not in taken.get(key[1], [])]
+                if not all(len(taken.get(key[1], [])) < SLOTS[key[1]] or users[taken[key[1]][-SLOTS[key[1]]]] == 0 for key in fresh):
+                    continue
+                for key in fresh:
+                    taken[key[1]] = taken.get(key[1], []) + [key]
+                emit()
+                done.add(n)
+                for key in tiles:
+                    users[key] = users[key] - 1
+                at[q] = at[q] + 1
+                moved = True
+        assert all(at[q] == len(queues[q]) for q in range(4)), [queues[q][at[q] : at[q] + 1] for q in range(4)]

@@ -434,9 +434,9 @@ def tile_infoncemi_pa_kernel(
 
         stream = ["110", 0, "111", 1, "112", 2, "113", 3, "203", 4, "210", 5, "211", 6, "212", 7, "213", 8, 9, 10, 11, 12, 13, 14, 15, 16, 17, 18, 19]
         extra = {"111": ["wq:200"], "113": ["xq:1"], "203": ["wq:201", "yn"], 4: ["yb"], "210": ["yd:0"], 5: ["wq:202", "yd:1"], "211": ["yd:2"], 6: ["yd:3", "md:00"],
-                 "212": ["md:01"], 7: ["md:02"], "213": ["md:03", "yv"], 10: pr("00"), 11: ["p1:01", "p2:01"], 12: ["a1:01", "a2:01", "p1:02", "p2:02"], 13: [],
-                 14: ["md:10", "p1:03", "p2:03"], 15: ["md:11", "a1:03", "a2:03"], 16: ["md:12"], 17: ["md:13"], 18: pr("20"), 19: pr("21")}
-        vector = ["wr:100a", "wq:100a", "xq:0", "wr:100b", "bc", "wq:100b", "wr:101", "wq:101", "wr:102", "wq:102", "wr:103", "wq:103"]
+                 "212": ["md:01"], 7: ["md:02"], "213": ["md:03", "yv"], 10: pr("00"), 11: ["p1:01", "p2:01"], 12: ["a1:01", "a2:01", "p1:02"], 13: [],
+                 14: ["md:10", "p2:02"], 15: ["md:11", "p1:03", "p2:03"], 16: ["md:12", "a1:03"], 17: ["md:13", "a2:03"], 18: pr("20"), 19: pr("21")}
+        vector = ["wr:100a", "wr:100b", "wq:100a", "xq:0", "wq:100b", "bc", "wr:101", "wq:101", "wr:102", "wq:102", "wr:103", "wq:103"]
 
         def stage(kind, item):
             return ("w" if item in LOADS else "h") + kind + ":" + (item if item in LOADS else name[item])
@@ -452,7 +452,7 @@ def tile_infoncemi_pa_kernel(
                          15: ["lx:03", "me:10"], 16: ["me:11", "ms:10"], 17: ["me:12", "ms:11"], 18: ["me:13", "ms:12"], 19: ["lt:20", "lt:21", "lx:20", "lx:21", "ms:13", "rs:0"]}
         tensor_behind = {3: ["xt:10", "xt:11"], 4: ["yt:0", "yt:1", "yt:2", "ys"], 5: ["yt:3", "yp"],
                          8: l2("000") + l2("001"), 9: l2("002"), 10: l2("003"), 11: l2("100"), 12: l2("101"), 13: l2("102"), 14: l2("103"),
-                         15: l2("010") + rd("01"), 16: l2("011"), 17: l2("012"), 18: l2("013") + l2("120"), 19: l2("121") + rd("03")}
+                         15: l2("010") + ["r1:01"], 16: l2("011"), 17: ["r2:01"] + l2("012"), 18: l2("013") + l2("120"), 19: l2("121") + rd("03")}
         tensor = ["xt:00", "xt:01", "bt"]
         scalar = ["xc:00", "xc:01"]
         for u in range(len(UNITS)):
@@ -464,7 +464,7 @@ def tile_infoncemi_pa_kernel(
             scalar += (["lt:" + following] if following is not None else []) + ["lx:" + n]
         for n in rest:
             vector += pr(n)
-        tensor += l2("122") + l2("123") + l2("130") + l2("131") + l2("132") + l2("133") + rd("21") + rd("23")
+        tensor += l2("122") + l2("123") + l2("130") + l2("131") + l2("132") + rd("21") + l2("133") + rd("23")
         tensor += rd("31") + rd("33")
         scalar += ["rs:2", "rs:3"]
 

@@ -28,7 +28,7 @@ UNITS = [(head, g, b) for head, b in ORDER for g in range(4)]
 CHUNKS = [(1, MU, 0, 256), (1, MU, 256, 256)] + [(1, MU, s, 512) for s in (512, 1024, 1536)] + [
     (layer, head, s, 512) for layer, head in ((1, LV), (2, MU), (2, LV)) for s in (0, 512, 1024, 1536)
 ]
-ON_SCALAR = ((2, MU, 0, 512), (2, MU, 512, 512), (2, MU, 1024, 512))
+ON_SCALAR = ((1, MU, 256, 256), (2, MU, 0, 512), (2, MU, 512, 512), (2, MU, 1024, 512))
 PAIRED = ((0, 1), (0, 3), (2, 1), (2, 3), (3, 1), (3, 3))
 LATE = ((LV, 2), (LV, 3))
 LOADS = ("x00", "x01", "100a", "100b", "101", "102", "103", "110", "200", "x1", "111", "112", "y0", "y1", "201", "113", "203", "202", "210", "211", "212", "213")
@@ -169,7 +169,7 @@ def tile_infoncemi_pa_kernel(
             nc.tensor.transpose(rot(("bias_t", "red"), [P, P], BF16)[:], btile[:], ident_bf[:])
 
         def bias_copy():
-            nc.vector.tensor_copy(out=bias_sb[:], in_=real["bias_t"][:, 0:40])
+            nc.scalar.copy(out=bias_sb[:], in_=real["bias_t"][:, 0:40])
 
         job("bt", [], [("bias_t", "red")], bias_transpose)
         job("bc", ["bt"], [("bias_t", "red")], bias_copy)
@@ -432,11 +432,11 @@ def tile_infoncemi_pa_kernel(
 
         sync = ["ld:" + n for n in LOADS] + ["st:0", "st:2", "st:3"]
 
-        stream = ["110", 0, "111", 1, "112", 2, "113", 3, "203", 4, "210", 5, "211", 6, "212", 7, "213", 8, 9, 10, 11, 12, 13, 14, 15, 16, 17, 18, 19]
+        stream = ["103", "110", 0, "111", 1, "112", 2, "113", 3, "203", 4, "210", 5, "211", 6, "212", 7, "213", 8, 9, 10, 11, 12, 13, 14, 15, 16, 17, 18, 19]
         extra = {"111": ["wq:200"], "113": ["xq:1"], "203": ["wq:201", "yn"], 4: ["yb"], "210": ["yd:0"], 5: ["wq:202", "yd:1"], "211": ["yd:2"], 6: ["yd:3", "md:00"],
                  "212": ["md:01"], 7: ["md:02"], "213": ["md:03", "yv"], 10: pr("00"), 11: ["p1:01", "p2:01"], 12: ["a1:01", "a2:01", "p1:02"], 13: [],
                  14: ["md:10", "p2:02"], 15: ["md:11", "p1:03", "p2:03"], 16: ["md:12", "a1:03"], 17: ["md:13", "a2:03"], 18: pr("20"), 19: pr("21")}
-        vector = ["wr:100a", "wr:100b", "wq:100a", "xq:0", "wq:100b", "bc", "wr:101", "wq:101", "wr:102", "wq:102", "wr:103", "wq:103"]
+        vector = ["wr:100a", "wq:100a", "xq:0", "wr:101", "wq:100b", "wq:101", "wr:102", "wq:102"]
 
         def stage(kind, item):
             return ("w" if item in LOADS else "h") + kind + ":" + (item if item in LOADS else name[item])
@@ -447,14 +447,14 @@ def tile_infoncemi_pa_kernel(
             vector += ahead + [stage("q", item)] + extra.get(item, [])
 
         scalar_behind = {2: ["wr:200"], 3: ["xc:10", "xc:11", "wr:201"], 4: ["yc:0", "yc:1"], 5: ["yc:2", "yc:3"], 6: ["wr:202"],
-                         8: ["me:00", "me:01"], 9: ["ms:00", "me:02", "ms:01"], 10: ["me:03", "ms:02"],
-                         11: ["ms:03"] + th("00"), 12: th("01"), 13: ["lt:02"], 14: ["lx:02", "lt:03"],
+                         8: ["me:00", "me:01"], 9: ["ms:00", "me:02"], 10: ["ms:01", "me:03"],
+                         11: ["ms:02", "ms:03"] + th("00"), 12: th("01"), 13: ["lt:02"], 14: ["lx:02", "lt:03"],
                          15: ["lx:03", "me:10"], 16: ["me:11", "ms:10"], 17: ["me:12", "ms:11"], 18: ["me:13", "ms:12"], 19: ["lt:20", "lt:21", "lx:20", "lx:21", "ms:13", "rs:0"]}
-        tensor_behind = {3: ["xt:10", "xt:11"], 4: ["yt:0", "yt:1", "yt:2", "ys"], 5: ["yt:3", "yp"],
+        tensor_behind = {3: ["xt:10", "xt:11"], 4: ["yt:0", "yt:1", "yt:2", "ys"], 5: ["yt:3"], 6: ["yp"],
                          8: l2("000") + l2("001"), 9: l2("002"), 10: l2("003"), 11: l2("100"), 12: l2("101"), 13: l2("102"), 14: l2("103"),
-                         15: l2("010") + ["r1:01"], 16: l2("011"), 17: ["r2:01"] + l2("012"), 18: l2("013") + l2("120"), 19: l2("121") + rd("03")}
+                         15: l2("010") + ["r1:01"], 16: l2("011"), 17: l2("012") + ["r2:01"], 18: l2("013") + l2("120"), 19: l2("121") + rd("03")}
         tensor = ["xt:00", "xt:01", "bt"]
-        scalar = ["xc:00", "xc:01"]
+        scalar = ["xc:00", "xc:01", "bc", "wr:100b"]
         for u in range(len(UNITS)):
             tensor += l1(u) + tensor_behind.get(u, [])
             scalar += ex(u) + scalar_behind.get(u, [])
@@ -462,8 +462,9 @@ def tile_infoncemi_pa_kernel(
         scalar += ["lt:" + rest[0]]
         for n, following in zip(rest, rest[1:] + [None]):
             scalar += (["lt:" + following] if following is not None else []) + ["lx:" + n]
-        for n in rest:
+        for n in rest[:-2]:
             vector += pr(n)
+        vector += ["p1:32", "p1:33", "p2:32", "a1:33", "p2:33", "a2:33"]
         tensor += l2("122") + l2("123") + l2("130") + l2("131") + l2("132") + rd("21") + l2("133") + rd("23")
         tensor += rd("31") + rd("33")
         scalar += ["rs:2", "rs:3"]

@@ -31,7 +31,7 @@ CHUNKS = [(1, MU, 0, 256), (1, MU, 256, 256)] + [(1, MU, s, 512) for s in (512, 
 ON_SCALAR = ((1, MU, 256, 256), (2, MU, 0, 512), (2, MU, 512, 512), (2, MU, 1024, 512))
 PAIRED = ((0, 1), (0, 3), (2, 1), (2, 3), (3, 1), (3, 3))
 LATE = ((LV, 2), (LV, 3))
-LOADS = ("x00", "x01", "100a", "100b", "101", "102", "103", "110", "200", "x1", "111", "112", "y0", "y1", "201", "113", "203", "202", "210", "211", "212", "213")
+LOADS = ("x00", "x01", "100a", "100b", "101", "102", "103", "bias", "110", "200", "x1", "111", "112", "y0", "y1", "201", "113", "203", "202", "210", "211", "212", "213")
 STEP = 1
 BEHIND = {(MU, 0): 6, (MU, 1): 3, (LV, 0): 4, (LV, 2): 2, (LV, 3): 4}
 
@@ -73,9 +73,8 @@ def tile_infoncemi_pa_kernel(
         btile = const.tile([P, P], BF16)
         nc.vector.memset(btile[:], 0.0)
         nc.scalar.dma_start(out=btile[0:16, :], in_=mu_b1.rearrange("(r p) -> r p", p=P))
-        nc.scalar.dma_start(out=btile[16:32, :], in_=lv_b1.rearrange("(r p) -> r p", p=P))
-        nc.scalar.dma_start(out=btile[32:36, :], in_=mu_b2.rearrange("(r p) -> r p", p=P))
-        nc.scalar.dma_start(out=btile[36:40, :], in_=lv_b2.rearrange("(r p) -> r p", p=P))
+        btile2 = const.tile([P, P], BF16)
+        nc.vector.memset(btile2[:], 0.0)
         warm = const.tile([P, 1], F32)
         nc.vector.memset(warm[:], 0.0)
         warm2 = const.tile([P, 1], F32)
@@ -127,6 +126,11 @@ def tile_infoncemi_pa_kernel(
         def quantise(codes, plane, grouped):
             nc.vector.quantize_mx(out=codes.bitcast(FP8X4), scales=plane, in_=grouped)
 
+        def bias_load():
+            nc.sync.dma_start(out=btile2[0:16, :], in_=lv_b1.rearrange("(r p) -> r p", p=P))
+            nc.sync.dma_start(out=btile2[16:20, :], in_=mu_b2.rearrange("(r p) -> r p", p=P))
+            nc.sync.dma_start(out=btile2[20:24, :], in_=lv_b2.rearrange("(r p) -> r p", p=P))
+
         def load_rows(tile, src, r0, rows):
             nc.sync.dma_start(
                 out=tile[:, r0 * 512 : (r0 + rows) * 512].rearrange("p (r k) -> p r k", r=rows),
@@ -169,7 +173,17 @@ def tile_infoncemi_pa_kernel(
             nc.tensor.transpose(rot(("bias_t", "red"), [P, P], BF16)[:], btile[:], ident_bf[:])
 
         def bias_copy():
-            nc.scalar.copy(out=bias_sb[:], in_=real["bias_t"][:, 0:40])
+            nc.scalar.copy(out=bias_sb[:, 0:16], in_=real["bias_t"][:, 0:16])
+
+        def bias_transpose_2():
+            nc.tensor.transpose(rot(("bias_u", "red"), [P, P], BF16)[:], btile2[:], ident_bf[:])
+
+        def bias_copy_2():
+            nc.scalar.copy(out=bias_sb[:, 16:40], in_=real["bias_u"][:, 0:24])
+
+        job("ld:bias", [], [], bias_load)
+        job("bt2", ["ld:bias"], [("bias_u", "red")], bias_transpose_2)
+        job("bc2", ["bt2"], [("bias_u", "red")], bias_copy_2)
 
         job("bt", [], [("bias_t", "red")], bias_transpose)
         job("bc", ["bt"], [("bias_t", "red")], bias_copy)
@@ -252,7 +266,7 @@ def tile_infoncemi_pa_kernel(
         job("yp", ["ld:y0", "ld:y1"], [("yprod", "l2")], y_products)
         job("ys", ["ld:y0", "ld:y1"], [("ytot", "red")], y_sums)
         job("yn", ["ys"], [("ytot", "red")], y_centre)
-        job("yb", ["yn", "bc"], [], y_bias)
+        job("yb", ["yn", "bc2"], [], y_bias)
         job("yv", ["yb"] + ["yd:%d" % dt for dt in range(4)], [], y_variance)
 
         def w_regroup(c):
@@ -302,7 +316,7 @@ def tile_infoncemi_pa_kernel(
                 bank = ("a%s%d" % (u, t), "l1")
                 needs = ["wq:1%d%d" % (head, g) + ("ab"[t // 2] if head == MU and g == 0 else ""), "xq:%d" % (BLOCKS[b][0] // 512)]
                 job("l1:%s:%d" % (u, t), needs, [bank], lambda unit=unit, t=t: l1_pass(unit, t))
-                job("ex:%s:%d" % (u, t), ["l1:%s:%d" % (u, t), "bc"], [bank, ("hpl" + u, "hpl")], lambda unit=unit, t=t: l1_exit(unit, t))
+                job("ex:%s:%d" % (u, t), ["l1:%s:%d" % (u, t), "bc" if head == MU else "bc2"], [bank, ("hpl" + u, "hpl")], lambda unit=unit, t=t: l1_exit(unit, t))
             job("hr:" + u, ["ex:%s:%d" % (u, t) for t in range(4)], [("hpl" + u, "hpl"), ("hg" + u, "hg")], lambda unit=unit: h_regroup(unit))
             job("hq:" + u, ["hr:" + u], [("hg" + u, "hg")], lambda unit=unit: h_quantise(unit))
 
@@ -446,11 +460,11 @@ def tile_infoncemi_pa_kernel(
             ahead = [stage("r", following)] if following is not None else []
             vector += ahead + [stage("q", item)] + extra.get(item, [])
 
-        scalar_behind = {2: ["wr:200"], 3: ["xc:10", "xc:11", "wr:201"], 4: ["yc:0", "yc:1"], 5: ["yc:2", "yc:3"], 6: ["wr:202"],
+        scalar_behind = {2: ["wr:200"], 3: ["bc2", "xc:10", "xc:11", "wr:201"], 4: ["yc:0", "yc:1"], 5: ["yc:2", "yc:3"], 6: ["wr:202"],
                          8: ["me:00", "me:01"], 9: ["ms:00", "me:02"], 10: ["ms:01", "me:03"],
                          11: ["ms:02", "ms:03"] + th("00"), 12: th("01"), 13: ["lt:02"], 14: ["lx:02", "lt:03"],
                          15: ["lx:03", "me:10"], 16: ["me:11", "ms:10"], 17: ["me:12", "ms:11"], 18: ["me:13", "ms:12"], 19: ["lt:20", "lt:21", "lx:20", "lx:21", "ms:13", "rs:0"]}
-        tensor_behind = {3: ["xt:10", "xt:11"], 4: ["yt:0", "yt:1", "yt:2", "ys"], 5: ["yt:3"], 6: ["yp"],
+        tensor_behind = {3: ["bt2", "xt:10", "xt:11"], 4: ["yt:0", "yt:1", "yt:2", "ys"], 5: ["yt:3"], 6: ["yp"],
                          8: l2("000") + l2("001"), 9: l2("002"), 10: l2("003"), 11: l2("100"), 12: l2("101"), 13: l2("102"), 14: l2("103"),
                          15: l2("010") + ["r1:01"], 16: l2("011"), 17: l2("012") + ["r2:01"], 18: l2("013") + l2("120"), 19: l2("121") + rd("03")}
         tensor = ["xt:00", "xt:01", "bt"]

@@ -121,7 +121,7 @@ def tile_infoncemi_pa_kernel(
                 hs[(head, b)] = keep.tile([P, 4 * BLOCKS[b][1]], U8, align_bytes=64, name="hs%d%d" % (head, b))
 
         def regroup(copy, dst, src):
-            copy(out=dst.rearrange("p (c i t) -> p c t i", i=4, t=4), in_=src.rearrange("p (t c i) -> p c t i", t=4, i=4))
+            copy(out=dst.rearrange("p (c i t) -> p c t i", i=8, t=4), in_=src.rearrange("p (t c i) -> p c t i", t=4, i=8))
 
         def quantise(codes, plane, grouped):
             nc.vector.quantize_mx(out=codes.bitcast(FP8X4), scales=plane, in_=grouped)
@@ -461,9 +461,8 @@ def tile_infoncemi_pa_kernel(
             vector += ahead + [stage("q", item)] + extra.get(item, [])
 
         scalar_behind = {2: ["wr:200"], 3: ["bc2", "xc:10", "xc:11", "wr:201"], 4: ["yc:0", "yc:1"], 5: ["yc:2", "yc:3"], 6: ["wr:202"],
-                         8: ["me:00", "me:01"], 9: ["ms:00", "me:02"], 10: ["ms:01", "me:03"],
-                         11: ["ms:02", "ms:03"] + th("00"), 12: th("01"), 13: ["lt:02"], 14: ["lx:02", "lt:03"],
-                         15: ["lx:03", "me:10"], 16: ["me:11", "ms:10"], 17: ["me:12", "ms:11"], 18: ["me:13", "ms:12"], 19: ["lt:20", "lt:21", "lx:20", "lx:21", "ms:13", "rs:0"]}
+                         8: ["me:00", "me:01"], 9: ["ms:00", "me:02"], 10: ["me:03", "ms:01"], 11: ["ms:02", "lt:00", "ms:03", "lx:00"], 12: ["lt:01"], 13: ["lx:01", "lt:02"], 14: ["lx:02", "lt:03"], 15: ["lx:03", "me:10"],
+                         16: ["me:11", "ms:10"], 17: ["me:12", "ms:11"], 18: ["me:13", "ms:12"], 19: ["lt:20", "lt:21", "lx:20", "lx:21", "ms:13", "rs:0"]}
         tensor_behind = {3: ["bt2", "xt:10", "xt:11"], 4: ["yt:0", "yt:1", "yt:2", "ys"], 5: ["yt:3"], 6: ["yp"],
                          8: l2("000") + l2("001"), 9: l2("002"), 10: l2("003"), 11: l2("100"), 12: l2("101"), 13: l2("102"), 14: l2("103"),
                          15: l2("010") + ["r1:01"], 16: l2("011"), 17: l2("012") + ["r2:01"], 18: l2("013") + l2("120"), 19: l2("121") + rd("03")}

@@ -69,7 +69,7 @@ def tile_infoncemi_pa_kernel(
                     real[name] = pools[tag].tile(shape, dtype, tag=slot, name=name, align_bytes=align)
             return real[name]
 
-        ctx.enter_context(tc.manual_schedule())
+        ctx.enter_context(tc.manual_schedule(engines={mybir.EngineType.SP}))
         btile = const.tile([P, P], BF16)
         nc.vector.memset(btile[:], 0.0)
         nc.scalar.dma_start(out=btile[0:16, :], in_=mu_b1.rearrange("(r p) -> r p", p=P))
@@ -491,25 +491,31 @@ def tile_infoncemi_pa_kernel(
         done = set()
         taken = {}
         at = [0, 0, 0, 0]
-        moved = True
-        while moved:
-            moved = False
-            for q, queue in enumerate(queues):
-                if at[q] >= len(queue):
-                    continue
-                n = queue[at[q]]
-                needs, tiles, emit = jobs[n]
-                if not all(m in done for m in needs):
-                    continue
-                fresh = [key for key in tiles if key not in taken.get(key[1], [])]
-                if not all(len(taken.get(key[1], [])) < SLOTS[key[1]] or users[taken[key[1]][-SLOTS[key[1]]]] == 0 for key in fresh):
-                    continue
-                for key in fresh:
-                    taken[key[1]] = taken.get(key[1], []) + [key]
-                emit()
-                done.add(n)
-                for key in tiles:
-                    users[key] = users[key] - 1
-                at[q] = at[q] + 1
-                moved = True
+
+        def write(until):
+            moved = True
+            while moved and until not in done:
+                moved = False
+                for q, queue in enumerate(queues):
+                    if at[q] >= len(queue):
+                        continue
+                    n = queue[at[q]]
+                    needs, tiles, emit = jobs[n]
+                    if not all(m in done for m in needs):
+                        continue
+                    fresh = [key for key in tiles if key not in taken.get(key[1], [])]
+                    if not all(len(taken.get(key[1], [])) < SLOTS[key[1]] or users[taken[key[1]][-SLOTS[key[1]]]] == 0 for key in fresh):
+                        continue
+                    for key in fresh:
+                        taken[key[1]] = taken.get(key[1], []) + [key]
+                    emit()
+                    done.add(n)
+                    for key in tiles:
+                        users[key] = users[key] - 1
+                    at[q] = at[q] + 1
+                    moved = True
+
+        with tc.manual_schedule(engines={mybir.EngineType.PE, mybir.EngineType.Activation, mybir.EngineType.DVE}):
+            write("xt:11")
+        write("")
         assert all(at[q] == len(queues[q]) for q in range(4)), [queues[q][at[q] : at[q] + 1] for q in range(4)]

@@ -29,7 +29,7 @@ CHUNKS = [(1, MU, 0, 256), (1, MU, 256, 256)] + [(1, MU, s, 512) for s in (512, 
     (layer, head, s, 512) for layer, head in ((1, LV), (2, MU), (2, LV)) for s in (0, 512, 1024, 1536)
 ]
 ON_SCALAR = ((1, MU, 256, 256), (2, MU, 0, 512), (2, MU, 512, 512), (2, MU, 1024, 512))
-PAIRED = ((0, 1), (0, 3), (2, 1), (2, 3), (3, 1), (3, 3))
+PAIRED = ((0, 3), (2, 1), (2, 3), (3, 1), (3, 3))
 LATE = ((LV, 2), (LV, 3))
 LOADS = ("x00", "x01", "100a", "100b", "101", "102", "103", "bias", "110", "200", "x1", "111", "112", "y0", "y1", "201", "113", "203", "202", "210", "211", "212", "213")
 STEP = 1
@@ -448,7 +448,7 @@ def tile_infoncemi_pa_kernel(
 
         stream = ["103", "110", 0, "111", 1, "112", 2, "113", 3, "203", 4, "210", 5, "211", 6, "212", 7, "213", 8, 9, 10, 11, 12, 13, 14, 15, 16, 17, 18, 19]
         extra = {"111": ["wq:200"], "113": ["xq:1"], "203": ["wq:201", "yn"], 4: ["yb"], "210": ["yd:0"], 5: ["wq:202", "yd:1"], "211": ["yd:2"], 6: ["yd:3", "md:00"],
-                 "212": ["md:01"], 7: ["md:02"], "213": ["md:03", "yv"], 10: pr("00"), 11: ["p1:01", "p2:01"], 12: ["a1:01", "a2:01", "p1:02"], 13: [],
+                 "212": ["md:01"], 7: ["md:02"], "213": ["md:03", "yv"], 10: pr("00"), 11: ["p1:01", "p2:01"], 12: ["p1:02"], 13: [],
                  14: ["md:10", "p2:02"], 15: ["md:11", "p1:03", "p2:03"], 16: ["md:12", "a1:03"], 17: ["md:13", "a2:03"], 18: pr("20"), 19: pr("21")}
         vector = ["wr:100a", "wq:100a", "xq:0", "wr:101", "wq:100b", "wq:101", "wr:102", "wq:102"]
 
@@ -464,8 +464,8 @@ def tile_infoncemi_pa_kernel(
                          8: ["me:00", "me:01"], 9: ["ms:00", "me:02"], 10: ["me:03", "ms:01"], 11: ["ms:02", "lt:00", "ms:03", "lx:00"], 12: ["lt:01"], 13: ["lx:01", "lt:02"], 14: ["lx:02", "lt:03"], 15: ["lx:03", "me:10"],
                          16: ["me:11", "ms:10"], 17: ["me:12", "ms:11"], 18: ["me:13", "ms:12"], 19: ["lt:20", "lt:21", "lx:20", "lx:21", "ms:13", "rs:0"]}
         tensor_behind = {3: ["bt2", "xt:10", "xt:11"], 4: ["yt:0", "yt:1", "yt:2", "ys"], 5: ["yt:3"], 6: ["yp"],
-                         8: l2("000") + l2("001"), 9: l2("002"), 10: l2("003"), 11: l2("100"), 12: l2("101"), 13: l2("102"), 14: l2("103"),
-                         15: l2("010") + ["r1:01"], 16: l2("011"), 17: l2("012") + ["r2:01"], 18: l2("013") + l2("120"), 19: l2("121") + rd("03")}
+                         8: l2("000") + l2("001"), 9: l2("002"), 10: l2("003"), 11: l2("100"), 12: l2("101"), 13: l2("102") + ["r1:00"], 14: l2("103"),
+                         15: l2("010") + ["r2:00"], 16: l2("011") + ["r1:01"], 17: l2("012") + ["r2:01"], 18: l2("013") + l2("120"), 19: l2("121") + rd("03")}
         tensor = ["xt:00", "xt:01", "bt"]
         scalar = ["xc:00", "xc:01", "bc", "wr:100b"]
         for u in range(len(UNITS)):

@@ -121,7 +121,7 @@ def tile_infoncemi_pa_kernel(
                 hs[(head, b)] = keep.tile([P, 4 * BLOCKS[b][1]], U8, align_bytes=64, name="hs%d%d" % (head, b))
 
         def regroup(copy, dst, src):
-            copy(out=dst.rearrange("p (c i t) -> p c t i", i=8, t=4), in_=src.rearrange("p (t c i) -> p c t i", t=4, i=8))
+            copy(out=dst.rearrange("p (c i t) -> p c t i", i=2, t=4), in_=src.rearrange("p (t c i) -> p c t i", t=4, i=2))
 
         def quantise(codes, plane, grouped):
             nc.vector.quantize_mx(out=codes.bitcast(FP8X4), scales=plane, in_=grouped)

from contextlib import ExitStack

import concourse.mybir as mybir
from concourse.masks import make_identity

FLOPS = 4 * 2 * 1024 * 512 * 2048

BF16 = mybir.dt.bfloat16
F32 = mybir.dt.float32
U32 = mybir.dt.uint32
U8 = mybir.dt.uint8
FP8X4 = mybir.dt.float8_e4m3fn_x4
ACT = mybir.ActivationFunctionType
ALU = mybir.AluOpType

P = 128
NS = 1024
MU = 0
LV = 1

SLOTS = {"xbig": 1, "wraw": 5, "wraws": 2, "grp": 2, "grps": 1, "hpl": 5, "hg": 2, "l1": 4, "l2": 3, "red": 1,
         "dlt": 3, "th": 2, "wgt": 4, "p1": 3, "p2": 3}

BLOCKS = ((0, 512), (512, 512), (512, 256), (768, 256))
OF_HEAD = {MU: (0, 1), LV: (0, 2, 3)}
ORDER = ((MU, 0), (LV, 0), (MU, 1), (LV, 2), (LV, 3))
UNITS = [(head, g, b) for head, b in ORDER for g in range(4)]
CHUNKS = [(1, MU, 0, 256), (1, MU, 256, 256)] + [(1, MU, s, 512) for s in (512, 1024, 1536)] + [
    (layer, head, s, 512) for layer, head in ((1, LV), (2, MU), (2, LV)) for s in (0, 512, 1024, 1536)
]
ON_SCALAR = ((1, MU, 256, 256), (2, MU, 0, 512), (2, MU, 512, 512), (2, MU, 1024, 512))
PAIRED = ((0, 3), (2, 1), (2, 3), (3, 1), (3, 3))
LATE = ((LV, 2), (LV, 3))
LOADS = ("x00", "x01", "100a", "100b", "101", "102", "103", "bias", "110", "200", "x1", "111", "112", "y0", "y1", "201", "113", "203", "202", "210", "211", "212", "213")
STEP = 1
BEHIND = {(MU, 0): 6, (MU, 1): 3, (LV, 0): 4, (LV, 2): 2, (LV, 3): 4}


def tile_infoncemi_pa_kernel(
    tc, x_samples, y_samples, mu_W1, mu_b1, mu_W2, mu_b2, lv_W1, lv_b1, lv_W2, lv_b2, out_0, out_1
):
    nc = tc.nc
    w_dram = {(1, MU): mu_W1, (1, LV): lv_W1, (2, MU): mu_W2, (2, LV): lv_W2}
    outs = (out_0, out_1)
    jobs = {}

    def job(name, needs, tiles, emit):
        jobs[name] = (needs, tiles, emit)

    with ExitStack() as ctx:
        const = ctx.enter_context(tc.tile_pool(name="const", bufs=1))
        keep = ctx.enter_context(tc.tile_pool(name="keep", bufs=1))
        pools = {}
        for tag in ("xbig", "wraw", "wraws", "grp", "grps", "hpl", "hg", "dlt", "th", "wgt", "p1", "p2"):
            pools[tag] = ctx.enter_context(tc.tile_pool(name="pool_" + tag, bufs=1))
        for tag in ("l1", "l2", "red"):
            pools[tag] = ctx.enter_context(tc.psum_pool(name="psum_" + tag, bufs=1))
        real = {}
        turn = {}

        def rot(key, shape, dtype, align=None):
            name, tag = key
            if name not in real:
                turn[tag] = turn.get(tag, -1) + 1
                slot = "%s_%d" % (tag, turn[tag] % SLOTS[tag])
                if align is None:
                    real[name] = pools[tag].tile(shape, dtype, tag=slot, name=name)
                else:
                    real[name] = pools[tag].tile(shape, dtype, tag=slot, name=name, align_bytes=align)
            return real[name]

        ctx.enter_context(tc.manual_schedule(engines={mybir.EngineType.SP}))
        btile = const.tile([P, P], BF16)
        nc.vector.memset(btile[:], 0.0)
        nc.scalar.dma_start(out=btile[0:16, :], in_=mu_b1.rearrange("(r p) -> r p", p=P))
        btile2 = const.tile([P, P], BF16)
        nc.vector.memset(btile2[:], 0.0)
        warm = const.tile([P, 1], F32)
        nc.vector.memset(warm[:], 0.0)
        warm2 = const.tile([P, 1], F32)
        nc.scalar.activation(out=warm2[:], in_=warm[:], func=ACT.Tanh)
        ident_f = const.tile([P, P], F32)
        make_identity(nc, ident_f[:])
        ident_bf = const.tile([P, P], BF16)
        make_identity(nc, ident_bf[:])
        sel = []
        for which, value in ((0, -0.5), (1, -0.5 / NS)):
            s = const.tile([P, P], F32, name="sel%d" % which)
            nc.vector.memset(s[:], 0.0)
            nc.vector.memset(s[:, which : which + 1], value)
            sel.append(s)
        ones = const.tile([P, 2], BF16)
        nc.vector.memset(ones[:], 1.0)
        bias_sb = const.tile([P, 40], F32)
        negc = const.tile([P, 4], F32)
        csq = const.tile([P, 4], F32)
        ebias = const.tile([P, 4], F32)
        vsum = const.tile([P, 4], F32)
        vn = const.tile([P, 4], F32)
        junk = const.tile([P, P], F32)

        xc = keep.tile([P, 1024], U32, align_bytes=64)
        xs = keep.tile([P, 1024], U8, align_bytes=64)
        y_raw = keep.tile([P, 4096], BF16)
        y_t = keep.tile([P, 4096], BF16)
        sq_d = keep.tile([P, 4096], F32)
        res = {}
        for b in OF_HEAD[LV]:
            res[b] = keep.tile([P, BLOCKS[b][1]], F32, name="res%d" % b)
        wc = {}
        ws = {}
        hc = {}
        hs = {}
        for layer in (1, 2):
            for head in (MU, LV):
                wc[(layer, head)] = keep.tile([P, 2048], U32, align_bytes=64, name="wc%d%d" % (layer, head))
                ws[(layer, head)] = keep.tile([P, 2048], U8, align_bytes=64, name="ws%d%d" % (layer, head))
        for head in (MU, LV):
            for b in OF_HEAD[head]:
                hc[(head, b)] = keep.tile([P, 4 * BLOCKS[b][1]], U32, align_bytes=64, name="hc%d%d" % (head, b))
                hs[(head, b)] = keep.tile([P, 4 * BLOCKS[b][1]], U8, align_bytes=64, name="hs%d%d" % (head, b))

        def regroup(copy, dst, src):
            copy(out=dst.rearrange("p (c i t) -> p c t i", i=2, t=4), in_=src.rearrange("p (t c i) -> p c t i", t=4, i=2))

        def quantise(codes, plane, grouped):
            nc.vector.quantize_mx(out=codes.bitcast(FP8X4), scales=plane, in_=grouped)

        def bias_load():
            nc.sync.dma_start(out=btile2[0:16, :], in_=lv_b1.rearrange("(r p) -> r p", p=P))
            nc.sync.dma_start(out=btile2[16:20, :], in_=mu_b2.rearrange("(r p) -> r p", p=P))
            nc.sync.dma_start(out=btile2[20:24, :], in_=lv_b2.rearrange("(r p) -> r p", p=P))

        def load_rows(tile, src, r0, rows):
            nc.sync.dma_start(
                out=tile[:, r0 * 512 : (r0 + rows) * 512].rearrange("p (r k) -> p r k", r=rows),
                in_=src[r0 * P : (r0 + rows) * P, :].rearrange("(r p) k -> p r k", p=P),
            )

        def x_all():
            return rot(("x", "xbig"), [P, 8192], BF16, 64)

        def sq_e():
            return rot(("sq_e", "xbig"), [P, 4096], F32, 64)

        def wname(c):
            return "%d%d%d" % (c[0], c[1], c[2] // 512) + ("" if c[3] == 512 else "ab"[c[2] // 256])

        def wkey(kind, c):
            return (kind + wname(c), kind + "s" if c in ON_SCALAR else kind)

        def w_load(c):
            layer, head, s, w = c
            raw = rot(wkey("wraw", c), [P, 4 * w], BF16)
            r3 = raw[:].rearrange("p (t c) -> p t c", t=4)
            if layer == 1:
                src = w_dram[(1, head)].rearrange("(u q e) c -> u q e c", u=2, e=2)
                for u in range(2):
                    nc.sync.dma_start(out=r3[:, 2 * u : 2 * u + 2, :], in_=src[u, :, :, s : s + w])
            else:
                nc.sync.dma_start(
                    out=r3, in_=w_dram[(2, head)][s : s + w, :].rearrange("(t p) d -> p t d", p=P)
                )

        for half in range(2):
            job("ld:y%d" % half, [], [], lambda half=half: load_rows(y_raw, y_samples, 4 * half, 4))
        for n, r0, rows in (("x00", 0, 2), ("x01", 2, 2), ("x1", 4, 4)):
            job("ld:" + n, [], [("x", "xbig")], lambda r0=r0, rows=rows: load_rows(x_all(), x_samples, r0, rows))
        for c in CHUNKS:
            job("ld:" + wname(c), [], [wkey("wraw", c)], lambda c=c: w_load(c))

        def bias_transpose():
            nc.tensor.transpose(rot(("bias_t", "red"), [P, P], BF16)[:], btile[:], ident_bf[:])

        def bias_copy():
            nc.scalar.copy(out=bias_sb[:, 0:16], in_=real["bias_t"][:, 0:16])

        def bias_transpose_2():
            nc.tensor.transpose(rot(("bias_u", "red"), [P, P], BF16)[:], btile2[:], ident_bf[:])

        def bias_copy_2():
            nc.scalar.copy(out=bias_sb[:, 16:40], in_=real["bias_u"][:, 0:24])

        job("ld:bias", [], [], bias_load)
        job("bt2", ["ld:bias"], [("bias_u", "red")], bias_transpose_2)
        job("bc2", ["bt2"], [("bias_u", "red")], bias_copy_2)

        job("bt", [], [("bias_t", "red")], bias_transpose)
        job("bc", ["bt"], [("bias_t", "red")], bias_copy)

        def x_transposes(half, pair):
            r0 = half * 4 + pair * 2
            xt = rot(("xt%d%d" % (half, pair), "l1"), [P, 512], F32)
            words = x_all()[:, 0:4096].bitcast(F32)
            for rr in range(2):
                for u in range(2):
                    nc.tensor.transpose(
                        xt[:, (rr * 2 + u) * P : (rr * 2 + u + 1) * P],
                        words[:, (r0 + rr) * 256 + u * P : (r0 + rr) * 256 + (u + 1) * P],
                        ident_f[:],
                    )

        def x_copy(half, pair):
            r0 = half * 4 + pair * 2
            nc.scalar.copy(
                out=x_all()[:, 4096:8192].bitcast(F32)[:, r0 * 256 : r0 * 256 + 512].rearrange("p (r n u) -> p r n u", r=2, u=2),
                in_=real["xt%d%d" % (half, pair)][:].rearrange("p (r u n) -> p r n u", r=2, u=2),
            )

        def x_quantise(half):
            sl = slice(half * 512, (half + 1) * 512)
            quantise(xc[:, sl], xs[:, sl], x_all()[:, 4096 + half * 2048 : 4096 + (half + 1) * 2048])

        for half in range(2):
            for pair in range(2):
                bank = ("xt%d%d" % (half, pair), "l1")
                job("xt:%d%d" % (half, pair), ["ld:x0%d" % pair if half == 0 else "ld:x1"], [bank, ("x", "xbig")], lambda half=half, pair=pair: x_transposes(half, pair))
                job("xc:%d%d" % (half, pair), ["xt:%d%d" % (half, pair)], [bank, ("x", "xbig")], lambda half=half, pair=pair: x_copy(half, pair))
            job("xq:%d" % half, ["xc:%d0" % half, "xc:%d1" % half], [("x", "xbig")], lambda half=half: x_quantise(half))

        def y_transposes(dt):
            yps = rot(("yps%d" % dt, "l2"), [P, 1024], BF16)
            for r in range(8):
                nc.tensor.transpose(
                    yps[:, r * P : (r + 1) * P], y_raw[:, r * 512 + dt * P : r * 512 + (dt + 1) * P], ident_bf[:]
                )

        def y_copy(dt):
            nc.scalar.copy(out=y_t[:, dt * 1024 : (dt + 1) * 1024], in_=real["yps%d" % dt][:])

        def y_products():
            prod = rot(("yprod", "l2"), [P, 512], F32)
            for dt in range(4):
                for r in range(8):
                    sl = slice(r * 512 + dt * P, r * 512 + (dt + 1) * P)
                    nc.tensor.matmul(out=prod[:, dt * P : (dt + 1) * P], lhsT=y_raw[:, sl], rhs=y_raw[:, sl],
                                     start=(r == 0), stop=(r == 7))

        def y_sums():
            tot = rot(("ytot", "red"), [P, 8], F32)
            for dt in range(4):
                for r in range(8):
                    sl = slice(r * 512 + dt * P, r * 512 + (dt + 1) * P)
                    nc.tensor.matmul(out=tot[:, 2 * dt : 2 * dt + 2], lhsT=y_raw[:, sl], rhs=ones[:],
                                     start=(r == 0), stop=(r == 7))

        def y_centre():
            nc.vector.tensor_scalar(out=negc[:], in0=real["ytot"][:].rearrange("p (d w) -> p d w", w=2)[:, :, 0],
                                    scalar1=-1.0 / NS, scalar2=None, op0=ALU.mult)

        def y_diagonal(dt):
            nc.vector.scalar_tensor_tensor(out=junk[:], in0=real["yprod"][:, dt * P : (dt + 1) * P], scalar=1.0 / NS,
                                           in1=ident_f[:], op0=ALU.mult, op1=ALU.mult, accum_out=vsum[:, dt : dt + 1])

        def y_bias():
            nc.vector.tensor_tensor(out=ebias[:], in0=bias_sb[:, 32:36], in1=negc[:], op=ALU.add)
            nc.vector.tensor_tensor(out=csq[:], in0=negc[:], in1=negc[:], op=ALU.mult)

        def y_variance():
            nc.vector.tensor_tensor(out=vn[:], in0=vsum[:], in1=csq[:], op=ALU.subtract)

        for dt in range(4):
            job("yt:%d" % dt, ["ld:y0", "ld:y1"], [("yps%d" % dt, "l2")], lambda dt=dt: y_transposes(dt))
            job("yc:%d" % dt, ["yt:%d" % dt], [("yps%d" % dt, "l2")], lambda dt=dt: y_copy(dt))
            job("yd:%d" % dt, ["yp"], [("yprod", "l2")], lambda dt=dt: y_diagonal(dt))
        job("yp", ["ld:y0", "ld:y1"], [("yprod", "l2")], y_products)
        job("ys", ["ld:y0", "ld:y1"], [("ytot", "red")], y_sums)
        job("yn", ["ys"], [("ytot", "red")], y_centre)
        job("yb", ["yn", "bc2"], [], y_bias)
        job("yv", ["yb"] + ["yd:%d" % dt for dt in range(4)], [], y_variance)

        def w_regroup(c):
            regroup(nc.scalar.copy if c in ON_SCALAR else nc.vector.tensor_copy, rot(wkey("grp", c), [P, 4 * c[3]], BF16, 64)[:], real[wkey("wraw", c)[0]][:])

        def w_quantise(c):
            layer, head, s, w = c
            sl = slice(s, s + w)
            quantise(wc[(layer, head)][:, sl], ws[(layer, head)][:, sl], real[wkey("grp", c)[0]][:])

        for c in CHUNKS:
            n = wname(c)
            job("wr:" + n, ["ld:" + n], [wkey("wraw", c), wkey("grp", c)], lambda c=c: w_regroup(c))
            job("wq:" + n, ["wr:" + n], [wkey("grp", c)], lambda c=c: w_quantise(c))

        def l1_pass(unit, t):
            head, g, b = unit
            first, w = BLOCKS[b]
            acc = rot(("a%d%d%d%d" % (head, g, b, t), "l1"), [P, w], F32)
            csl = slice(g * 512 + t * P, g * 512 + (t + 1) * P)
            nsl = slice(first, first + w)
            nc.tensor.matmul_mx(out=acc[:], lhsT=wc[(1, head)][:, csl].bitcast(FP8X4), lhsT_scale=ws[(1, head)][:, csl],
                                rhs=xc[:, nsl].bitcast(FP8X4), rhs_scale=xs[:, nsl], start=True, stop=True)

        def l1_exit(unit, t):
            head, g, b = unit
            w = BLOCKS[b][1]
            hpl = rot(("hpl%d%d%d" % unit, "hpl"), [P, 4 * w], BF16)
            col = head * 16 + g * 4 + t
            nc.scalar.activation(out=hpl[:, t * w : (t + 1) * w], in_=real["a%d%d%d%d" % (head, g, b, t)][:],
                                 func=ACT.Relu, bias=bias_sb[:, col : col + 1])

        def h_regroup(unit):
            w = BLOCKS[unit[2]][1]
            regroup(nc.vector.tensor_copy, rot(("hg%d%d%d" % unit, "hg"), [P, 4 * w], BF16, 64)[:], real["hpl%d%d%d" % unit][:])

        def h_quantise(unit):
            head, g, b = unit
            w = BLOCKS[b][1]
            sl = slice(g * w, (g + 1) * w)
            quantise(hc[(head, b)][:, sl], hs[(head, b)][:, sl], real["hg%d%d%d" % unit][:])

        for unit in UNITS:
            head, g, b = unit
            u = "%d%d%d" % unit
            for t in range(4):
                bank = ("a%s%d" % (u, t), "l1")
                needs = ["wq:1%d%d" % (head, g) + ("ab"[t // 2] if head == MU and g == 0 else ""), "xq:%d" % (BLOCKS[b][0] // 512)]
                job("l1:%s:%d" % (u, t), needs, [bank], lambda unit=unit, t=t: l1_pass(unit, t))
                job("ex:%s:%d" % (u, t), ["l1:%s:%d" % (u, t), "bc" if head == MU else "bc2"], [bank, ("hpl" + u, "hpl")], lambda unit=unit, t=t: l1_exit(unit, t))
            job("hr:" + u, ["ex:%s:%d" % (u, t) for t in range(4)], [("hpl" + u, "hpl"), ("hg" + u, "hg")], lambda unit=unit: h_regroup(unit))
            job("hq:" + u, ["hr:" + u], [("hg" + u, "hg")], lambda unit=unit: h_quantise(unit))

        def o_key(head, b, dt):
            return ("o%d%d%d" % (head, b, dt), "l1" if (head, b) in LATE and (b, dt) >= (2, 2) else "l2")

        def red_key(b):
            return ("red%d" % b, "l2" if b == 3 else "red")

        def l2_pass(head, b, dt, g):
            w = BLOCKS[b][1]
            acc = rot(o_key(head, b, dt), [P, w], F32)
            wsl = slice(g * 512 + dt * P, g * 512 + (dt + 1) * P)
            hsl = slice(g * w, (g + 1) * w)
            nc.tensor.matmul_mx(out=acc[:], lhsT=wc[(2, head)][:, wsl].bitcast(FP8X4), lhsT_scale=ws[(2, head)][:, wsl],
                                rhs=hc[(head, b)][:, hsl].bitcast(FP8X4), rhs_scale=hs[(head, b)][:, hsl],
                                start=(g == 0), stop=(g == 3))

        def cols(b, dt):
            first, w = BLOCKS[b]
            return slice(dt * 1024 + first, dt * 1024 + first + w)

        def mu_delta(b, dt):
            nc.vector.scalar_tensor_tensor(
                out=rot(("dlt%d%d" % (b, dt), "dlt"), [P, 512], F32)[:], in0=real["o%d%d%d" % (MU, b, dt)][:],
                scalar=bias_sb[:, 32 + dt : 33 + dt], in1=y_t[:, cols(b, dt)], op0=ALU.add, op1=ALU.subtract)

        def mu_centred_square(b, dt):
            nc.scalar.activation(out=sq_e()[:, cols(b, dt)], in_=real["o%d%d%d" % (MU, b, dt)][:], func=ACT.Square,
                                 bias=ebias[:, dt : dt + 1])

        def mu_delta_square(b, dt):
            nc.scalar.activation(out=sq_d[:, cols(b, dt)], in_=real["dlt%d%d" % (b, dt)][:], func=ACT.Square)

        def lv_tanh(b, dt):
            nc.scalar.activation(out=rot(("th%d%d" % (b, dt), "th"), [P, BLOCKS[b][1]], F32)[:],
                                 in_=real["o%d%d%d" % (LV, b, dt)][:], func=ACT.Tanh, bias=bias_sb[:, 36 + dt : 37 + dt])

        def lv_exp(b, dt):
            nc.scalar.activation(out=rot(("wgt%d%d" % (b, dt), "wgt"), [P, BLOCKS[b][1]], F32)[:],
                                 in_=real["th%d%d" % (b, dt)][:], func=ACT.Exp, scale=-1.0)

        def product(which, b, dt):
            out = rot(("p%d%d%d" % (which, b, dt), "p%d" % which), [P, BLOCKS[b][1]], F32)
            if which == 1:
                nc.vector.tensor_tensor(out=out[:], in0=sq_d[:, cols(b, dt)], in1=real["wgt%d%d" % (b, dt)][:], op=ALU.mult)
            else:
                nc.vector.scalar_tensor_tensor(out=out[:], in0=sq_e()[:, cols(b, dt)], scalar=vn[:, dt : dt + 1],
                                               in1=real["wgt%d%d" % (b, dt)][:], op0=ALU.add, op1=ALU.mult)

        def pair_sum(which, b, dt):
            here = real["p%d%d%d" % (which, b, dt)][:]
            nc.vector.tensor_tensor(out=here, in0=real["p%d%d%d" % (which, b, dt - 1)][:], in1=here, op=ALU.add)

        def reduce_d(which, b, dt, first, last):
            nc.tensor.matmul(out=rot(red_key(b), [P, BLOCKS[b][1]], F32)[:], lhsT=sel[which - 1][:],
                             rhs=real["p%d%d%d" % (which, b, dt)][:], start=first, stop=last)

        def result(b):
            nc.scalar.copy(out=res[b][:], in_=real["red%d" % b][:])

        def store(b):
            first, w = BLOCKS[b]
            for which in range(2):
                nc.sync.dma_start(out=outs[which][first : first + w].rearrange("(o n) -> o n", o=1), in_=res[b][which : which + 1, :])

        for head in (MU, LV):
            for b in OF_HEAD[head]:
                for dt in range(4):
                    n = "%d%d" % (b, dt)
                    for g in range(4):
                        job("l2:%d%s:%d" % (head, n, g), ["wq:2%d%d" % (head, g), "hq:%d%d%d" % (head, g, b)] + ["l2:%d%s:%d" % (head, n, g - 1)] * (g > 0), [o_key(head, b, dt)],
                            lambda head=head, b=b, dt=dt, g=g: l2_pass(head, b, dt, g))
        for b in OF_HEAD[MU]:
            for dt in range(4):
                n = "%d%d" % (b, dt)
                mk = o_key(MU, b, dt)
                job("md:" + n, ["l2:0%s:3" % n, "yc:%d" % dt], [mk, ("dlt" + n, "dlt")], lambda b=b, dt=dt: mu_delta(b, dt))
                job("me:" + n, ["l2:0%s:3" % n, "yb"], [mk, ("sq_e", "xbig")], lambda b=b, dt=dt: mu_centred_square(b, dt))
                job("ms:" + n, ["md:" + n], [("dlt" + n, "dlt")], lambda b=b, dt=dt: mu_delta_square(b, dt))
        reduces = {}
        for b in OF_HEAD[LV]:
            reduces[b] = [(which, dt) for dt in range(4) for which in (1, 2) if (b, dt + 1) not in PAIRED]
            for dt in range(4):
                n = "%d%d" % (b, dt)
                m = "%d%d" % (BLOCKS[b][0] // 512, dt)
                wk = ("wgt" + n, "wgt")
                job("lt:" + n, ["l2:1%s:3" % n], [o_key(LV, b, dt), ("th" + n, "th")], lambda b=b, dt=dt: lv_tanh(b, dt))
                job("lx:" + n, ["lt:" + n], [("th" + n, "th"), wk], lambda b=b, dt=dt: lv_exp(b, dt))
                job("p1:" + n, ["lx:" + n, "ms:" + m], [wk, ("p1" + n, "p1")], lambda b=b, dt=dt: product(1, b, dt))
                job("p2:" + n, ["lx:" + n, "me:" + m, "yv"], [wk, ("p2" + n, "p2"), ("sq_e", "xbig")], lambda b=b, dt=dt: product(2, b, dt))
                for which in (1, 2):
                    last = ["p%d:%s" % (which, n)]
                    if (b, dt) in PAIRED:
                        before = "%d%d" % (b, dt - 1)
                        job("a%d:%s" % (which, n), ["p%d:%s" % (which, before)] + last,
                            [("p%d%s" % (which, before), "p%d" % which), ("p%d%s" % (which, n), "p%d" % which)],
                            lambda which=which, b=b, dt=dt: pair_sum(which, b, dt))
                        last = ["a%d:%s" % (which, n)]
                    if (which, dt) in reduces[b]:
                        at = reduces[b].index((which, dt))
                        last = last + ["r%d:%d%d" % (reduces[b][at - 1][0], b, reduces[b][at - 1][1])] * (at > 0)
                        job("r%d:%s" % (which, n), last, [("p%d%s" % (which, n), "p%d" % which), red_key(b)],
                            lambda which=which, b=b, dt=dt, at=at: reduce_d(which, b, dt, at == 0, at == len(reduces[b]) - 1))
            job("rs:%d" % b, ["r%d:%d%d" % (which, b, dt) for which, dt in reduces[b]], [red_key(b)], lambda b=b: result(b))
            job("st:%d" % b, ["rs:%d" % b], [], lambda b=b: store(b))

        name = ["%d%d%d" % unit for unit in UNITS]

        def l1(u):
            return ["l1:%s:%d" % (name[u], t) for t in range(4)]

        def ex(u):
            return ["ex:%s:%d" % (name[u], t) for t in range(4)]

        def l2(n):
            return ["l2:%s:%d" % (n, g) for g in range(4)]

        def th(n):
            return ["lt:" + n, "lx:" + n]

        def pr(n):
            return ["p1:" + n, "p2:" + n] + (["a1:" + n, "a2:" + n] if (int(n[0]), int(n[1])) in PAIRED else [])

        def rd(n):
            return ["r%d:%s" % (which, n) for which in (1, 2) if (which, int(n[1])) in reduces[int(n[0])]]

        sync = ["ld:" + n for n in LOADS] + ["st:0", "st:2", "st:3"]

        stream = ["103", "110", 0, "111", 1, "112", 2, "113", 3, "203", 4, "210", 5, "211", 6, "212", 7, "213", 8, 9, 10, 11, 12, 13, 14, 15, 16, 17, 18, 19]
        extra = {"111": ["wq:200"], "113": ["xq:1"], "203": ["wq:201", "yn"], 4: ["yb"], "210": ["yd:0"], 5: ["wq:202", "yd:1"], "211": ["yd:2"], 6: ["yd:3", "md:00"],
                 "212": ["md:01"], 7: ["md:02"], "213": ["md:03", "yv"], 10: pr("00"), 11: ["p1:01", "p2:01"], 12: ["p1:02"], 13: [],
                 14: ["md:10", "p2:02"], 15: ["md:11", "p1:03", "p2:03"], 16: ["md:12", "a1:03"], 17: ["md:13", "a2:03"], 18: pr("20"), 19: pr("21")}
        vector = ["wr:100a", "wq:100a", "xq:0", "wr:101", "wq:100b", "wq:101", "wr:102", "wq:102"]

        def stage(kind, item):
            return ("w" if item in LOADS else "h") + kind + ":" + (item if item in LOADS else name[item])

        vector += [stage("r", stream[0])]
        for item, following in zip(stream, stream[1:] + [None]):
            ahead = [stage("r", following)] if following is not None else []
            vector += ahead + [stage("q", item)] + extra.get(item, [])

        scalar_behind = {2: ["wr:200"], 3: ["bc2", "xc:10", "xc:11", "wr:201"], 4: ["yc:0", "yc:1"], 5: ["yc:2", "yc:3"], 6: ["wr:202"],
                         8: ["me:00", "me:01"], 9: ["ms:00", "me:02"], 10: ["me:03", "ms:01"], 11: ["ms:02", "lt:00", "ms:03", "lx:00"], 12: ["lt:01"], 13: ["lx:01", "lt:02"], 14: ["lx:02", "lt:03"], 15: ["lx:03", "me:10"],
                         16: ["me:11", "ms:10"], 17: ["me:12", "ms:11"], 18: ["me:13", "ms:12"], 19: ["lt:20", "lt:21", "lx:20", "lx:21", "ms:13", "rs:0"]}
        tensor_behind = {3: ["bt2", "xt:10", "xt:11"], 4: ["yt:0", "yt:1", "yt:2", "ys"], 5: ["yt:3"], 6: ["yp"],
                         8: l2("000") + l2("001"), 9: l2("002"), 10: l2("003"), 11: l2("100"), 12: l2("101"), 13: l2("102") + ["r1:00"], 14: l2("103"),
                         15: l2("010") + ["r2:00"], 16: l2("011") + ["r1:01"], 17: l2("012") + ["r2:01"], 18: l2("013") + l2("120"), 19: l2("121") + rd("03")}
        tensor = ["xt:00", "xt:01", "bt"]
        scalar = ["xc:00", "xc:01", "bc", "wr:100b"]
        for u in range(len(UNITS)):
            tensor += l1(u) + tensor_behind.get(u, [])
            scalar += ex(u) + scalar_behind.get(u, [])
        rest = ["22", "23", "30", "31", "32", "33"]
        scalar += ["lt:" + rest[0]]
        for n, following in zip(rest, rest[1:] + [None]):
            scalar += (["lt:" + following] if following is not None else []) + ["lx:" + n]
        for n in rest[:-2]:
            vector += pr(n)
        vector += ["p1:32", "p1:33", "p2:32", "a1:33", "p2:33", "a2:33"]
        tensor += l2("122") + l2("123") + l2("130") + l2("131") + l2("132") + rd("21") + l2("133") + rd("23")
        tensor += rd("31") + rd("33")
        scalar += ["rs:2", "rs:3"]

        queues = [sync, tensor, scalar, vector]
        users = {}
        for queue in queues:
            for n in queue:
                for key in jobs[n][1]:
                    users[key] = users.get(key, 0) + 1
        done = set()
        taken = {}
        at = [0, 0, 0, 0]

        def write(until):
            moved = True
            while moved and until not in done:
                moved = False
                for q, queue in enumerate(queues):
                    if at[q] >= len(queue):
                        continue
                    n = queue[at[q]]
                    needs, tiles, emit = jobs[n]
                    if not all(m in done for m in needs):
                        continue
                    fresh = [key for key in tiles if key not in taken.get(key[1], [])]
                    if not all(len(taken.get(key[1], [])) < SLOTS[key[1]] or users[taken[key[1]][-SLOTS[key[1]]]] == 0 for key in fresh):
                        continue
                    for key in fresh:
                        taken[key[1]] = taken.get(key[1], []) + [key]
                    emit()
                    done.add(n)
                    for key in tiles:
                        users[key] = users[key] - 1
                    at[q] = at[q] + 1
                    moved = True

        with tc.manual_schedule(engines={mybir.EngineType.PE, mybir.EngineType.Activation, mybir.EngineType.DVE}):
            write("xt:11")
        write("")
        assert all(at[q] == len(queues[q]) for q in range(4)), [queues[q][at[q] : at[q] + 1] for q in range(4)]
